import numpy as np
import ml_dtypes


def mxq(x, axis, fmt="e4m3"):
    dtype, down = {"e4m3": (ml_dtypes.float8_e4m3fn, 7), "e5m2": (ml_dtypes.float8_e5m2, 14)}[fmt]
    v = np.moveaxis(np.asarray(x, np.float32).astype(ml_dtypes.bfloat16).astype(np.float64), axis, -1)
    blocks = v.reshape(v.shape[:-1] + (-1, 32))
    amax = np.abs(blocks).max(-1, keepdims=True)
    byte = np.maximum(np.where(amax > 0, np.frexp(amax)[1] - 1 + 127, 0) - down, 1)
    scale = np.exp2(byte - 127.0)
    codes = (blocks / scale).astype(np.float32).astype(dtype).astype(np.float64)
    return np.moveaxis((codes * scale).reshape(v.shape), -1, axis)


WIDE = False


def mx_kscale(k):
    if not WIDE:
        return np.ones(k)
    levels = np.array([10, -10, 5, -5, 0])
    a = np.random.permutation(np.resize(levels, k // 512 * 4)).reshape(k // 512, 4)
    idx = np.arange(k)
    return np.exp2(a[idx // 512, idx % 128 // 32])


BF16 = ml_dtypes.bfloat16


def bf(x):
    return np.asarray(x, np.float32).astype(BF16)


def f64(x):
    return np.asarray(x).astype(np.float64)


N, C, H, W, HIDDEN, OUT = 8, 512, 16, 16, 512, 256
P = H * W
M = N * P


def leaky_relu(v):
    return np.where(v >= 0.0, v, 0.01 * v)


def setup_inputs():
    s, t = mx_kscale(M), mx_kscale(HIDDEN)
    strong = np.where(np.random.random((M, M)) * N < 1.0, 1.0, 0.02)
    weight = np.random.random((M, M)) * strong * 2.0 / P
    hid = leaky_relu(np.random.standard_normal((M, HIDDEN)) * 0.8 - 0.4)
    return {"weight": bf(weight * s[None, :]),
            "hid": bf(hid * t[None, :] / s[:, None]),
            "W2": bf(np.random.standard_normal((OUT, HIDDEN)) * 3.0 / np.sqrt(HIDDEN) / t[None, :]),
            "b2": bf(np.random.standard_normal(OUT) * 0.2 - 0.3)}


def reference(weight, hid, W2, b2):
    agg = mxq(f64(weight), 1, "e4m3") @ mxq(f64(hid), 0, "e4m3")
    y = leaky_relu((mxq(agg, 1, "e4m3") @ mxq(f64(W2), 1, "e4m3").T) + f64(b2))
    y = y.reshape(N, H, W, -1).transpose(0, 3, 1, 2)
    return y.max(axis=0, keepdims=True)

@@ -1,0 +1,211 @@
+import concourse.mybir as mybir
+from concourse.masks import make_identity
+
+F32 = mybir.dt.float32
+BF16 = mybir.dt.bfloat16
+U32 = mybir.dt.uint32
+U8 = mybir.dt.uint8
+FP8X4 = mybir.dt.float8_e4m3fn_x4
+ADD = mybir.AluOpType.add
+MULT = mybir.AluOpType.mult
+MAX = mybir.AluOpType.max
+
+P = 128
+PACK = 4
+K_PASS = P * PACK
+
+NODES = 2048
+HIDDEN = 512
+OUT = 256
+SAMPLES = 8
+PIXELS = NODES // SAMPLES
+NODE_PASSES = NODES // K_PASS
+ROW_TILES = PIXELS // P
+FEATURE_TILES = HIDDEN // P
+OUT_TILES = OUT // P
+HALVES = 2
+SLOPE = 0.01
+
+FLOPS = 2 * NODES * NODES * HIDDEN + 2 * NODES * HIDDEN * OUT
+
+
+def tile_similargcn_pb_kernel(tc, weight, hid, W2, b2, out):
+    nc = tc.nc
+    with (
+        tc.manual_schedule(),
+        tc.tile_pool(name="const", bufs=1) as const,
+        tc.tile_pool(name="w_in", bufs=SAMPLES) as w_in,
+        tc.tile_pool(name="w_work", bufs=2) as w_work,
+        tc.tile_pool(name="agg_work", bufs=2) as agg_work,
+        tc.psum_pool(name="psum_setup", bufs=1) as psum_setup,
+        tc.psum_pool(name="psum_wt", bufs=2 * ROW_TILES) as psum_wt,
+        tc.psum_pool(name="psum_agg", bufs=ROW_TILES) as psum_agg,
+        tc.psum_pool(name="psum_y", bufs=1) as psum_y,
+    ):
+        ident_f32 = const.tile([P, P], F32)
+        make_identity(nc, ident_f32[:])
+        ident_bf16 = const.tile([P, P], BF16)
+        make_identity(nc, ident_bf16[:])
+
+        w2_raw = const.tile([P, OUT_TILES, HIDDEN], BF16)
+        nc.scalar.dma_start(out=w2_raw[:], in_=W2.rearrange("(t p) f -> p t f", p=P))
+        bias_rows = const.tile([P, P], BF16)
+        nc.vector.memset(bias_rows[:], 0.0)
+        nc.scalar.dma_start(out=bias_rows[0:OUT_TILES, :], in_=b2.rearrange("(t o) -> t o", t=OUT_TILES))
+
+        hid_raw = const.tile([P, NODE_PASSES, PACK, HIDDEN], BF16)
+        for g in range(NODE_PASSES):
+            nc.sync.dma_start(
+                out=hid_raw[:, g, :, :].rearrange("p (u e) f -> p u e f", u=HALVES),
+                in_=hid[g * K_PASS : (g + 1) * K_PASS, :].rearrange("(u p e) f -> p u e f", u=HALVES, p=P),
+            )
+        w_raw = []
+        for n in range(SAMPLES):
+            rows = w_in.tile([P, ROW_TILES, NODES], BF16, name="w_raw")
+            nc.sync.dma_start(
+                out=rows[:], in_=weight[n * PIXELS : (n + 1) * PIXELS, :].rearrange("(j p) k -> p j k", p=P)
+            )
+            w_raw.append(rows)
+
+        w2_t = psum_setup.tile([P, OUT_TILES, FEATURE_TILES, P], BF16, tag="setup")
+        for t_o in range(OUT_TILES):
+            for t in range(FEATURE_TILES):
+                nc.tensor.transpose(w2_t[:, t_o, t, :], w2_raw[:, t_o, t * P : (t + 1) * P], ident_bf16[:])
+        w2_grouped = const.tile([P, OUT_TILES, P, PACK], BF16, align_bytes=64)
+        nc.vector.tensor_copy(out=w2_grouped[:], in_=w2_t[:].rearrange("p a t o -> p a o t"))
+        bias_t = psum_setup.tile([P, P], BF16, tag="setup")
+        nc.tensor.transpose(bias_t[:], bias_rows[:], ident_bf16[:])
+        bias = const.tile([P, OUT_TILES], F32)
+        nc.vector.tensor_copy(out=bias[:], in_=bias_t[:, 0:OUT_TILES])
+        w2_codes = const.tile([P, OUT], U32, align_bytes=64)
+        w2_scales = const.tile([P, OUT], U8, align_bytes=64)
+        nc.vector.quantize_mx(
+            out=w2_codes[:].bitcast(FP8X4),
+            scales=w2_scales[:],
+            in_=w2_grouped[:].rearrange("p a o t -> p (a o t)"),
+        )
+
+        hid_grouped = const.tile([P, NODE_PASSES, HIDDEN, PACK], BF16, align_bytes=64)
+        hid_codes = const.tile([P, NODE_PASSES, HIDDEN], U32, align_bytes=64)
+        hid_scales = const.tile([P, NODE_PASSES, HIDDEN], U8, align_bytes=64)
+        half = HIDDEN // 2
+        for g in range(NODE_PASSES):
+            nc.vector.tensor_copy(
+                out=hid_grouped[:, g, 0:half, :].rearrange("p (c i) t -> p c t i", i=4),
+                in_=hid_raw[:, g, :, 0:half].rearrange("p t (c i) -> p c t i", i=4),
+            )
+            nc.scalar.copy(
+                out=hid_grouped[:, g, half:HIDDEN, :].rearrange("p (c i) t -> p c t i", i=4),
+                in_=hid_raw[:, g, :, half:HIDDEN].rearrange("p t (c i) -> p c t i", i=4),
+            )
+            if g > 0:
+                quantise_hid(nc, hid_grouped, hid_codes, hid_scales, g - 1)
+        quantise_hid(nc, hid_grouped, hid_codes, hid_scales, NODE_PASSES - 1)
+
+        w_codes = {}
+        w_scales = {}
+        agg_codes = {}
+        agg_scales = {}
+        y_max = const.tile([P, OUT_TILES, PIXELS], F32)
+
+        def transpose_weight(n):
+            grouped = w_work.tile([P, ROW_TILES, NODE_PASSES * P * PACK], BF16, align_bytes=64, name="w_grouped")
+            codes = w_work.tile([P, ROW_TILES, NODE_PASSES * P], U32, align_bytes=64, name="w_codes")
+            scales = w_work.tile([P, ROW_TILES, NODE_PASSES * P], U8, align_bytes=64, name="w_scales")
+            banks = []
+            for j in range(ROW_TILES):
+                words = w_raw[n][:, j, :].bitcast(F32)
+                for b in range(2):
+                    w_t = psum_wt.tile([P, 2, HALVES, P], F32, name="w_t")
+                    for i in range(2):
+                        for u in range(HALVES):
+                            c0 = ((2 * b + i) * HALVES + u) * P
+                            nc.tensor.transpose(w_t[:, i, u, :], words[:, c0 : c0 + P], ident_f32[:])
+                    banks.append(w_t)
+            for j in range(ROW_TILES):
+                pairs = grouped[:, j, :].bitcast(F32).rearrange("p (b i m u) -> p b i m u", b=2, i=2, u=HALVES)
+                nc.scalar.copy(out=pairs[:, 0], in_=banks[2 * j][:].rearrange("p i u m -> p i m u"))
+                nc.vector.tensor_copy(out=pairs[:, 1], in_=banks[2 * j + 1][:].rearrange("p i u m -> p i m u"))
+            for j in range(ROW_TILES):
+                nc.vector.quantize_mx(out=codes[:, j, :].bitcast(FP8X4), scales=scales[:, j, :], in_=grouped[:, j, :])
+            w_codes[n] = codes
+            w_scales[n] = scales
+
+        def aggregate(n):
+            grouped = agg_work.tile([P, ROW_TILES, P, PACK], BF16, align_bytes=64, name="agg_grouped")
+            codes = agg_work.tile([P, PIXELS], U32, align_bytes=64, name="agg_codes")
+            scales = agg_work.tile([P, PIXELS], U8, align_bytes=64, name="agg_scales")
+            for j in range(ROW_TILES):
+                agg_t = psum_agg.tile([P, FEATURE_TILES, P], F32, name="agg_t")
+                for t in range(FEATURE_TILES):
+                    for g in range(NODE_PASSES):
+                        nc.tensor.matmul_mx(
+                            out=agg_t[:, t, :],
+                            lhsT=hid_codes[:, g, t * P : (t + 1) * P].bitcast(FP8X4),
+                            lhsT_scale=hid_scales[:, g, t * P : (t + 1) * P],
+                            rhs=w_codes[n][:, j, g * P : (g + 1) * P].bitcast(FP8X4),
+                            rhs_scale=w_scales[n][:, j, g * P : (g + 1) * P],
+                            start=(g == 0),
+                            stop=(g == NODE_PASSES - 1),
+                        )
+                nc.scalar.copy(out=grouped[:, j, :, :], in_=agg_t[:].rearrange("p t m -> p m t"))
+            nc.vector.quantize_mx(
+                out=codes[:].bitcast(FP8X4), scales=scales[:], in_=grouped[:].rearrange("p j m t -> p (j m t)")
+            )
+            agg_codes[n] = codes
+            agg_scales[n] = scales
+
+        def project(n):
+            y_t = psum_y.tile([P, OUT_TILES, PIXELS], F32, name="y_t")
+            for t_o in range(OUT_TILES):
+                nc.tensor.matmul_mx(
+                    out=y_t[:, t_o, :],
+                    lhsT=w2_codes[:, t_o * P : (t_o + 1) * P].bitcast(FP8X4),
+                    lhsT_scale=w2_scales[:, t_o * P : (t_o + 1) * P],
+                    rhs=agg_codes[n][:].bitcast(FP8X4),
+                    rhs_scale=agg_scales[n][:],
+                    start=True,
+                    stop=True,
+                )
+            for t_o in range(OUT_TILES):
+                if n == 0:
+                    nc.vector.tensor_scalar_add(
+                        out=y_max[:, t_o, :], in0=y_t[:, t_o, :], scalar1=bias[:, t_o : t_o + 1]
+                    )
+                else:
+                    nc.vector.scalar_tensor_tensor(
+                        out=y_max[:, t_o, :],
+                        in0=y_t[:, t_o, :],
+                        scalar=bias[:, t_o : t_o + 1],
+                        in1=y_max[:, t_o, :],
+                        op0=ADD,
+                        op1=MAX,
+                    )
+
+        transpose_weight(0)
+        for n in range(SAMPLES):
+            if n + 1 < SAMPLES:
+                transpose_weight(n + 1)
+            aggregate(n)
+            if n > 0:
+                project(n - 1)
+        project(SAMPLES - 1)
+
+        result = const.tile([P, OUT_TILES, PIXELS], F32)
+        nc.vector.scalar_tensor_tensor(
+            out=result[:].rearrange("p t m -> p (t m)"),
+            in0=y_max[:].rearrange("p t m -> p (t m)"),
+            scalar=SLOPE,
+            in1=y_max[:].rearrange("p t m -> p (t m)"),
+            op0=MULT,
+            op1=MAX,
+        )
+        nc.sync.dma_start(out=out[0].rearrange("(t p) h w -> p t (h w)", p=P), in_=result[:])
+
+
+def quantise_hid(nc, hid_grouped, hid_codes, hid_scales, g):
+    nc.vector.quantize_mx(
+        out=hid_codes[:, g, :].bitcast(FP8X4),
+        scales=hid_scales[:, g, :],
+        in_=hid_grouped[:, g, :, :].rearrange("p f t -> p (f t)"),
+    )

@@ -24,6 +24,7 @@ ROW_TILES = PIXELS // P
 FEATURE_TILES = HIDDEN // P
 OUT_TILES = OUT // P
 HALVES = 2
+BANKS_PER_TILE = 2
 SLOPE = 0.01
 
 FLOPS = 2 * NODES * NODES * HIDDEN + 2 * NODES * HIDDEN * OUT
@@ -34,11 +35,10 @@ def tile_similargcn_pb_kernel(tc, weight, hid, W2, b2, out):
     with (
         tc.manual_schedule(),
         tc.tile_pool(name="const", bufs=1) as const,
-        tc.tile_pool(name="w_in", bufs=SAMPLES) as w_in,
+        tc.tile_pool(name="w_in", bufs=SAMPLES * ROW_TILES) as w_in,
         tc.tile_pool(name="w_work", bufs=2) as w_work,
         tc.tile_pool(name="agg_work", bufs=2) as agg_work,
-        tc.psum_pool(name="psum_setup", bufs=1) as psum_setup,
-        tc.psum_pool(name="psum_wt", bufs=2 * ROW_TILES) as psum_wt,
+        tc.psum_pool(name="psum_wt", bufs=BANKS_PER_TILE * ROW_TILES + 1) as psum_wt,
         tc.psum_pool(name="psum_agg", bufs=ROW_TILES) as psum_agg,
         tc.psum_pool(name="psum_y", bufs=1) as psum_y,
     ):
@@ -47,43 +47,25 @@ def tile_similargcn_pb_kernel(tc, weight, hid, W2, b2, out):
         ident_bf16 = const.tile([P, P], BF16)
         make_identity(nc, ident_bf16[:])
 
-        w2_raw = const.tile([P, OUT_TILES, HIDDEN], BF16)
-        nc.scalar.dma_start(out=w2_raw[:], in_=W2.rearrange("(t p) f -> p t f", p=P))
-        bias_rows = const.tile([P, P], BF16)
-        nc.vector.memset(bias_rows[:], 0.0)
-        nc.scalar.dma_start(out=bias_rows[0:OUT_TILES, :], in_=b2.rearrange("(t o) -> t o", t=OUT_TILES))
-
         hid_raw = const.tile([P, NODE_PASSES, PACK, HIDDEN], BF16)
         for g in range(NODE_PASSES):
             nc.sync.dma_start(
                 out=hid_raw[:, g, :, :].rearrange("p (u e) f -> p u e f", u=HALVES),
                 in_=hid[g * K_PASS : (g + 1) * K_PASS, :].rearrange("(u p e) f -> p u e f", u=HALVES, p=P),
             )
-        w_raw = []
+        w2_raw = const.tile([P, OUT_TILES, HIDDEN], BF16)
+        bias_rows = const.tile([P, P], BF16)
+        nc.vector.memset(bias_rows[:], 0.0)
+        w_raw = {}
         for n in range(SAMPLES):
-            rows = w_in.tile([P, ROW_TILES, NODES], BF16, name="w_raw")
-            nc.sync.dma_start(
-                out=rows[:], in_=weight[n * PIXELS : (n + 1) * PIXELS, :].rearrange("(j p) k -> p j k", p=P)
-            )
-            w_raw.append(rows)
-
-        w2_t = psum_setup.tile([P, OUT_TILES, FEATURE_TILES, P], BF16, tag="setup")
-        for t_o in range(OUT_TILES):
-            for t in range(FEATURE_TILES):
-                nc.tensor.transpose(w2_t[:, t_o, t, :], w2_raw[:, t_o, t * P : (t + 1) * P], ident_bf16[:])
-        w2_grouped = const.tile([P, OUT_TILES, P, PACK], BF16, align_bytes=64)
-        nc.vector.tensor_copy(out=w2_grouped[:], in_=w2_t[:].rearrange("p a t o -> p a o t"))
-        bias_t = psum_setup.tile([P, P], BF16, tag="setup")
-        nc.tensor.transpose(bias_t[:], bias_rows[:], ident_bf16[:])
-        bias = const.tile([P, OUT_TILES], F32)
-        nc.vector.tensor_copy(out=bias[:], in_=bias_t[:, 0:OUT_TILES])
-        w2_codes = const.tile([P, OUT], U32, align_bytes=64)
-        w2_scales = const.tile([P, OUT], U8, align_bytes=64)
-        nc.vector.quantize_mx(
-            out=w2_codes[:].bitcast(FP8X4),
-            scales=w2_scales[:],
-            in_=w2_grouped[:].rearrange("p a o t -> p (a o t)"),
-        )
+            for j in range(ROW_TILES):
+                rows = w_in.tile([P, NODES], BF16, name="w_raw")
+                r0 = n * PIXELS + j * P
+                nc.sync.dma_start(out=rows[:], in_=weight[r0 : r0 + P, :])
+                w_raw[n, j] = rows
+            if n == 1:
+                nc.sync.dma_start(out=w2_raw[:], in_=W2.rearrange("(t p) f -> p t f", p=P))
+                nc.sync.dma_start(out=bias_rows[0:OUT_TILES, :], in_=b2.rearrange("(t o) -> t o", t=OUT_TILES))
 
         hid_grouped = const.tile([P, NODE_PASSES, HIDDEN, PACK], BF16, align_bytes=64)
         hid_codes = const.tile([P, NODE_PASSES, HIDDEN], U32, align_bytes=64)
@@ -108,49 +90,75 @@ def tile_similargcn_pb_kernel(tc, weight, hid, W2, b2, out):
         agg_scales = {}
         y_max = const.tile([P, OUT_TILES, PIXELS], F32)
 
+        bias = const.tile([P, OUT_TILES], F32)
+        w2_codes = const.tile([P, OUT], U32, align_bytes=64)
+        w2_scales = const.tile([P, OUT], U8, align_bytes=64)
+
+        def prepare_w2():
+            w2_t = psum_wt.tile([P, OUT_TILES, FEATURE_TILES, P], BF16, tag="w_t")
+            for t_o in range(OUT_TILES):
+                for t in range(FEATURE_TILES):
+                    nc.tensor.transpose(w2_t[:, t_o, t, :], w2_raw[:, t_o, t * P : (t + 1) * P], ident_bf16[:])
+            bias_t = psum_wt.tile([P, P], BF16, tag="w_t")
+            nc.tensor.transpose(bias_t[:], bias_rows[:], ident_bf16[:])
+            w2_grouped = const.tile([P, OUT_TILES, P, PACK], BF16, align_bytes=64)
+            nc.vector.tensor_copy(out=w2_grouped[:], in_=w2_t[:].rearrange("p a t o -> p a o t"))
+            nc.vector.tensor_copy(out=bias[:], in_=bias_t[:, 0:OUT_TILES])
+            nc.vector.quantize_mx(
+                out=w2_codes[:].bitcast(FP8X4),
+                scales=w2_scales[:],
+                in_=w2_grouped[:].rearrange("p a o t -> p (a o t)"),
+            )
+
         def transpose_weight(n):
             grouped = w_work.tile([P, ROW_TILES, NODE_PASSES * P * PACK], BF16, align_bytes=64, name="w_grouped")
             codes = w_work.tile([P, ROW_TILES, NODE_PASSES * P], U32, align_bytes=64, name="w_codes")
             scales = w_work.tile([P, ROW_TILES, NODE_PASSES * P], U8, align_bytes=64, name="w_scales")
-            banks = []
             for j in range(ROW_TILES):
-                words = w_raw[n][:, j, :].bitcast(F32)
-                for b in range(2):
+                words = w_raw[n, j][:].bitcast(F32)
+                pairs = grouped[:, j, :].bitcast(F32).rearrange(
+                    "p (b i m u) -> p b i m u", b=BANKS_PER_TILE, i=2, u=HALVES
+                )
+                for b in range(BANKS_PER_TILE):
                     w_t = psum_wt.tile([P, 2, HALVES, P], F32, name="w_t")
                     for i in range(2):
                         for u in range(HALVES):
                             c0 = ((2 * b + i) * HALVES + u) * P
                             nc.tensor.transpose(w_t[:, i, u, :], words[:, c0 : c0 + P], ident_f32[:])
-                    banks.append(w_t)
-            for j in range(ROW_TILES):
-                pairs = grouped[:, j, :].bitcast(F32).rearrange("p (b i m u) -> p b i m u", b=2, i=2, u=HALVES)
-                nc.scalar.copy(out=pairs[:, 0], in_=banks[2 * j][:].rearrange("p i u m -> p i m u"))
-                nc.vector.tensor_copy(out=pairs[:, 1], in_=banks[2 * j + 1][:].rearrange("p i u m -> p i m u"))
-            for j in range(ROW_TILES):
+                    if b == 0:
+                        nc.scalar.copy(out=pairs[:, b], in_=w_t[:].rearrange("p i u m -> p i m u"))
+                    else:
+                        nc.vector.tensor_copy(out=pairs[:, b], in_=w_t[:].rearrange("p i u m -> p i m u"))
                 nc.vector.quantize_mx(out=codes[:, j, :].bitcast(FP8X4), scales=scales[:, j, :], in_=grouped[:, j, :])
             w_codes[n] = codes
             w_scales[n] = scales
 
-        def aggregate(n):
-            grouped = agg_work.tile([P, ROW_TILES, P, PACK], BF16, align_bytes=64, name="agg_grouped")
+        agg_grouped = {}
+
+        def aggregate(n, j):
+            if j == 0:
+                agg_grouped[n] = agg_work.tile([P, ROW_TILES, P, PACK], BF16, align_bytes=64, name="agg_grouped")
+            agg_t = psum_agg.tile([P, FEATURE_TILES, P], F32, name="agg_t")
+            for t in range(FEATURE_TILES):
+                for g in range(NODE_PASSES):
+                    nc.tensor.matmul_mx(
+                        out=agg_t[:, t, :],
+                        lhsT=hid_codes[:, g, t * P : (t + 1) * P].bitcast(FP8X4),
+                        lhsT_scale=hid_scales[:, g, t * P : (t + 1) * P],
+                        rhs=w_codes[n][:, j, g * P : (g + 1) * P].bitcast(FP8X4),
+                        rhs_scale=w_scales[n][:, j, g * P : (g + 1) * P],
+                        start=(g == 0),
+                        stop=(g == NODE_PASSES - 1),
+                    )
+            nc.scalar.copy(out=agg_grouped[n][:, j, :, :], in_=agg_t[:].rearrange("p t m -> p m t"))
+
+        def quantise_agg(n):
             codes = agg_work.tile([P, PIXELS], U32, align_bytes=64, name="agg_codes")
             scales = agg_work.tile([P, PIXELS], U8, align_bytes=64, name="agg_scales")
-            for j in range(ROW_TILES):
-                agg_t = psum_agg.tile([P, FEATURE_TILES, P], F32, name="agg_t")
-                for t in range(FEATURE_TILES):
-                    for g in range(NODE_PASSES):
-                        nc.tensor.matmul_mx(
-                            out=agg_t[:, t, :],
-                            lhsT=hid_codes[:, g, t * P : (t + 1) * P].bitcast(FP8X4),
-                            lhsT_scale=hid_scales[:, g, t * P : (t + 1) * P],
-                            rhs=w_codes[n][:, j, g * P : (g + 1) * P].bitcast(FP8X4),
-                            rhs_scale=w_scales[n][:, j, g * P : (g + 1) * P],
-                            start=(g == 0),
-                            stop=(g == NODE_PASSES - 1),
-                        )
-                nc.scalar.copy(out=grouped[:, j, :, :], in_=agg_t[:].rearrange("p t m -> p m t"))
             nc.vector.quantize_mx(
-                out=codes[:].bitcast(FP8X4), scales=scales[:], in_=grouped[:].rearrange("p j m t -> p (j m t)")
+                out=codes[:].bitcast(FP8X4),
+                scales=scales[:],
+                in_=agg_grouped[n][:].rearrange("p j m t -> p (j m t)"),
             )
             agg_codes[n] = codes
             agg_scales[n] = scales
@@ -184,9 +192,13 @@ def tile_similargcn_pb_kernel(tc, weight, hid, W2, b2, out):
 
         transpose_weight(0)
         for n in range(SAMPLES):
+            aggregate(n, 0)
             if n + 1 < SAMPLES:
                 transpose_weight(n + 1)
-            aggregate(n)
+            if n == 0:
+                prepare_w2()
+            aggregate(n, 1)
+            quantise_agg(n)
             if n > 0:
                 project(n - 1)
         project(SAMPLES - 1)

@@ -25,6 +25,7 @@ FEATURE_TILES = HIDDEN // P
 OUT_TILES = OUT // P
 HALVES = 2
 BANKS_PER_TILE = 2
+LEAD = 1
 SLOPE = 0.01
 
 FLOPS = 2 * NODES * NODES * HIDDEN + 2 * NODES * HIDDEN * OUT
@@ -111,14 +112,14 @@ def tile_similargcn_pb_kernel(tc, weight, hid, W2, b2, out):
             )
 
         def transpose_weight(n):
-            grouped = w_work.tile([P, ROW_TILES, NODE_PASSES * P * PACK], BF16, align_bytes=64, name="w_grouped")
-            codes = w_work.tile([P, ROW_TILES, NODE_PASSES * P], U32, align_bytes=64, name="w_codes")
-            scales = w_work.tile([P, ROW_TILES, NODE_PASSES * P], U8, align_bytes=64, name="w_scales")
+            grouped = w_work.tile([P, NODE_PASSES * PIXELS * PACK], BF16, align_bytes=64, name="w_grouped")
+            codes = w_work.tile([P, NODE_PASSES, PIXELS], U32, align_bytes=64, name="w_codes")
+            scales = w_work.tile([P, NODE_PASSES, PIXELS], U8, align_bytes=64, name="w_scales")
+            pairs = grouped[:].bitcast(F32).rearrange(
+                "p (b i j m u) -> p b j i m u", b=BANKS_PER_TILE, i=2, j=ROW_TILES, u=HALVES
+            )
             for j in range(ROW_TILES):
                 words = w_raw[n, j][:].bitcast(F32)
-                pairs = grouped[:, j, :].bitcast(F32).rearrange(
-                    "p (b i m u) -> p b i m u", b=BANKS_PER_TILE, i=2, u=HALVES
-                )
                 for b in range(BANKS_PER_TILE):
                     w_t = psum_wt.tile([P, 2, HALVES, P], F32, name="w_t")
                     for i in range(2):
@@ -126,39 +127,49 @@ def tile_similargcn_pb_kernel(tc, weight, hid, W2, b2, out):
                             c0 = ((2 * b + i) * HALVES + u) * P
                             nc.tensor.transpose(w_t[:, i, u, :], words[:, c0 : c0 + P], ident_f32[:])
                     if b == 0:
-                        nc.scalar.copy(out=pairs[:, b], in_=w_t[:].rearrange("p i u m -> p i m u"))
+                        nc.scalar.copy(out=pairs[:, b, j], in_=w_t[:].rearrange("p i u m -> p i m u"))
                     else:
-                        nc.vector.tensor_copy(out=pairs[:, b], in_=w_t[:].rearrange("p i u m -> p i m u"))
-                nc.vector.quantize_mx(out=codes[:, j, :].bitcast(FP8X4), scales=scales[:, j, :], in_=grouped[:, j, :])
+                        nc.vector.tensor_copy(out=pairs[:, b, j], in_=w_t[:].rearrange("p i u m -> p i m u"))
+            width = 2 * PIXELS * PACK
+            for b in range(BANKS_PER_TILE):
+                nc.vector.quantize_mx(
+                    out=codes[:, 2 * b : 2 * b + 2, :].rearrange("p g m -> p (g m)").bitcast(FP8X4),
+                    scales=scales[:, 2 * b : 2 * b + 2, :].rearrange("p g m -> p (g m)"),
+                    in_=grouped[:, b * width : (b + 1) * width],
+                )
             w_codes[n] = codes
             w_scales[n] = scales
 
         agg_grouped = {}
+        agg_bank = {}
 
-        def aggregate(n, j):
-            if j == 0:
-                agg_grouped[n] = agg_work.tile([P, ROW_TILES, P, PACK], BF16, align_bytes=64, name="agg_grouped")
-            agg_t = psum_agg.tile([P, FEATURE_TILES, P], F32, name="agg_t")
-            for t in range(FEATURE_TILES):
+        def aggregate(n, feature_tiles):
+            for t in feature_tiles:
+                h, s = divmod(t, 2)
+                if t == 0:
+                    agg_grouped[n] = agg_work.tile([P, PIXELS, PACK], BF16, align_bytes=64, name="agg_grouped")
+                if s == 0:
+                    agg_bank[n] = psum_agg.tile([P, 2, PIXELS], F32, name="agg_t")
                 for g in range(NODE_PASSES):
                     nc.tensor.matmul_mx(
-                        out=agg_t[:, t, :],
+                        out=agg_bank[n][:, s, :],
                         lhsT=hid_codes[:, g, t * P : (t + 1) * P].bitcast(FP8X4),
                         lhsT_scale=hid_scales[:, g, t * P : (t + 1) * P],
-                        rhs=w_codes[n][:, j, g * P : (g + 1) * P].bitcast(FP8X4),
-                        rhs_scale=w_scales[n][:, j, g * P : (g + 1) * P],
+                        rhs=w_codes[n][:, g, :].bitcast(FP8X4),
+                        rhs_scale=w_scales[n][:, g, :],
                         start=(g == 0),
                         stop=(g == NODE_PASSES - 1),
                     )
-            nc.scalar.copy(out=agg_grouped[n][:, j, :, :], in_=agg_t[:].rearrange("p t m -> p m t"))
+                if s == 1:
+                    nc.scalar.copy(
+                        out=agg_grouped[n][:, :, 2 * h : 2 * h + 2], in_=agg_bank[n][:].rearrange("p s m -> p m s")
+                    )
 
         def quantise_agg(n):
             codes = agg_work.tile([P, PIXELS], U32, align_bytes=64, name="agg_codes")
             scales = agg_work.tile([P, PIXELS], U8, align_bytes=64, name="agg_scales")
             nc.vector.quantize_mx(
-                out=codes[:].bitcast(FP8X4),
-                scales=scales[:],
-                in_=agg_grouped[n][:].rearrange("p j m t -> p (j m t)"),
+                out=codes[:].bitcast(FP8X4), scales=scales[:], in_=agg_grouped[n][:].rearrange("p m t -> p (m t)")
             )
             agg_codes[n] = codes
             agg_scales[n] = scales
@@ -192,15 +203,15 @@ def tile_similargcn_pb_kernel(tc, weight, hid, W2, b2, out):
 
         transpose_weight(0)
         for n in range(SAMPLES):
-            aggregate(n, 0)
+            aggregate(n, range(0, LEAD))
             if n + 1 < SAMPLES:
                 transpose_weight(n + 1)
             if n == 0:
                 prepare_w2()
-            aggregate(n, 1)
-            quantise_agg(n)
+            aggregate(n, range(LEAD, FEATURE_TILES))
             if n > 0:
                 project(n - 1)
+            quantise_agg(n)
         project(SAMPLES - 1)
 
         result = const.tile([P, OUT_TILES, PIXELS], F32)

@@ -24,9 +24,9 @@ ROW_TILES = PIXELS // P
 FEATURE_TILES = HIDDEN // P
 OUT_TILES = OUT // P
 HALVES = 2
-BANKS_PER_TILE = 2
-LEAD = 1
+LAST = SAMPLES - 1
 SLOPE = 0.01
+COPIERS = "SVSV"
 
 FLOPS = 2 * NODES * NODES * HIDDEN + 2 * NODES * HIDDEN * OUT
 
@@ -36,12 +36,11 @@ def tile_similargcn_pb_kernel(tc, weight, hid, W2, b2, out):
     with (
         tc.manual_schedule(),
         tc.tile_pool(name="const", bufs=1) as const,
-        tc.tile_pool(name="w_in", bufs=SAMPLES * ROW_TILES) as w_in,
-        tc.tile_pool(name="w_work", bufs=2) as w_work,
+        tc.tile_pool(name="w_in", bufs=SAMPLES) as w_in,
+        tc.tile_pool(name="w_work", bufs=3) as w_work,
         tc.tile_pool(name="agg_work", bufs=2) as agg_work,
-        tc.psum_pool(name="psum_wt", bufs=BANKS_PER_TILE * ROW_TILES + 1) as psum_wt,
-        tc.psum_pool(name="psum_agg", bufs=ROW_TILES) as psum_agg,
-        tc.psum_pool(name="psum_y", bufs=1) as psum_y,
+        tc.psum_pool(name="psum_wt", bufs=4) as psum_wt,
+        tc.psum_pool(name="psum_acc", bufs=4) as psum_acc,
     ):
         ident_f32 = const.tile([P, P], F32)
         make_identity(nc, ident_f32[:])
@@ -57,13 +56,18 @@ def tile_similargcn_pb_kernel(tc, weight, hid, W2, b2, out):
         w2_raw = const.tile([P, OUT_TILES, HIDDEN], BF16)
         bias_rows = const.tile([P, P], BF16)
         nc.vector.memset(bias_rows[:], 0.0)
-        w_raw = {}
+        w_raw = []
         for n in range(SAMPLES):
-            for j in range(ROW_TILES):
-                rows = w_in.tile([P, NODES], BF16, name="w_raw")
-                r0 = n * PIXELS + j * P
-                nc.sync.dma_start(out=rows[:], in_=weight[r0 : r0 + P, :])
-                w_raw[n, j] = rows
+            rows = w_in.tile([P, ROW_TILES, NODES], BF16, name="w_raw")
+            chunks = 2 if n < 2 else 1
+            width = NODES // chunks
+            for c in range(chunks):
+                cols = slice(c * width, (c + 1) * width)
+                nc.sync.dma_start(
+                    out=rows[:, :, cols],
+                    in_=weight[n * PIXELS : (n + 1) * PIXELS, cols].rearrange("(j p) k -> p j k", p=P),
+                )
+            w_raw.append(rows)
             if n == 1:
                 nc.sync.dma_start(out=w2_raw[:], in_=W2.rearrange("(t p) f -> p t f", p=P))
                 nc.sync.dma_start(out=bias_rows[0:OUT_TILES, :], in_=b2.rearrange("(t o) -> t o", t=OUT_TILES))
@@ -72,7 +76,8 @@ def tile_similargcn_pb_kernel(tc, weight, hid, W2, b2, out):
         hid_codes = const.tile([P, NODE_PASSES, HIDDEN], U32, align_bytes=64)
         hid_scales = const.tile([P, NODE_PASSES, HIDDEN], U8, align_bytes=64)
         half = HIDDEN // 2
-        for g in range(NODE_PASSES):
+
+        def regroup_hid(g):
             nc.vector.tensor_copy(
                 out=hid_grouped[:, g, 0:half, :].rearrange("p (c i) t -> p c t i", i=4),
                 in_=hid_raw[:, g, :, 0:half].rearrange("p t (c i) -> p c t i", i=4),
@@ -81,19 +86,28 @@ def tile_similargcn_pb_kernel(tc, weight, hid, W2, b2, out):
                 out=hid_grouped[:, g, half:HIDDEN, :].rearrange("p (c i) t -> p c t i", i=4),
                 in_=hid_raw[:, g, :, half:HIDDEN].rearrange("p t (c i) -> p c t i", i=4),
             )
-            if g > 0:
-                quantise_hid(nc, hid_grouped, hid_codes, hid_scales, g - 1)
-        quantise_hid(nc, hid_grouped, hid_codes, hid_scales, NODE_PASSES - 1)
 
-        w_codes = {}
-        w_scales = {}
-        agg_codes = {}
-        agg_scales = {}
+        def quantise_hid(g):
+            nc.vector.quantize_mx(
+                out=hid_codes[:, g, :].bitcast(FP8X4),
+                scales=hid_scales[:, g, :],
+                in_=hid_grouped[:, g, :, :].rearrange("p f t -> p (f t)"),
+            )
+
         y_max = const.tile([P, OUT_TILES, PIXELS], F32)
-
         bias = const.tile([P, OUT_TILES], F32)
         w2_codes = const.tile([P, OUT], U32, align_bytes=64)
         w2_scales = const.tile([P, OUT], U8, align_bytes=64)
+        result = const.tile([P, OUT_TILES, PIXELS], F32)
+        w_banks = {}
+        w_grouped = {}
+        w_codes = {}
+        w_scales = {}
+        agg_banks = {}
+        agg_grouped = {}
+        agg_codes = {}
+        agg_scales = {}
+        y_banks = {}
 
         def prepare_w2():
             w2_t = psum_wt.tile([P, OUT_TILES, FEATURE_TILES, P], BF16, tag="w_t")
@@ -112,123 +126,161 @@ def tile_similargcn_pb_kernel(tc, weight, hid, W2, b2, out):
             )
 
         def transpose_weight(n):
-            grouped = w_work.tile([P, NODE_PASSES * PIXELS * PACK], BF16, align_bytes=64, name="w_grouped")
-            codes = w_work.tile([P, NODE_PASSES, PIXELS], U32, align_bytes=64, name="w_codes")
-            scales = w_work.tile([P, NODE_PASSES, PIXELS], U8, align_bytes=64, name="w_scales")
-            pairs = grouped[:].bitcast(F32).rearrange(
-                "p (b i j m u) -> p b j i m u", b=BANKS_PER_TILE, i=2, j=ROW_TILES, u=HALVES
+            w_grouped[n] = w_work.tile([P, NODE_PASSES, PIXELS, PACK], BF16, align_bytes=64, name="w_grouped")
+            w_codes[n] = w_work.tile([P, NODE_PASSES, PIXELS], U32, align_bytes=64, name="w_codes")
+            w_scales[n] = w_work.tile([P, NODE_PASSES, PIXELS], U8, align_bytes=64, name="w_scales")
+            for g in range(NODE_PASSES):
+                w_t = psum_wt.tile([P, ROW_TILES, HALVES, P], F32, name="w_t")
+                for j in range(ROW_TILES):
+                    words = w_raw[n][:, j, :].bitcast(F32)
+                    for u in range(HALVES):
+                        c0 = (g * HALVES + u) * P
+                        nc.tensor.transpose(w_t[:, j, u, :], words[:, c0 : c0 + P], ident_f32[:])
+                w_banks[n, g] = w_t
+
+        def copy_weight(n, g):
+            grouped = w_grouped[n][:, g, :, :].rearrange("p m t -> p (m t)").bitcast(F32)
+            copy = nc.scalar.copy if COPIERS[g] == "S" else nc.vector.tensor_copy
+            copy(
+                out=grouped.rearrange("p (j m u) -> p j m u", j=ROW_TILES, u=HALVES),
+                in_=w_banks[n, g][:].rearrange("p j u m -> p j m u"),
             )
-            for j in range(ROW_TILES):
-                words = w_raw[n, j][:].bitcast(F32)
-                for b in range(BANKS_PER_TILE):
-                    w_t = psum_wt.tile([P, 2, HALVES, P], F32, name="w_t")
-                    for i in range(2):
-                        for u in range(HALVES):
-                            c0 = ((2 * b + i) * HALVES + u) * P
-                            nc.tensor.transpose(w_t[:, i, u, :], words[:, c0 : c0 + P], ident_f32[:])
-                    if b == 0:
-                        nc.scalar.copy(out=pairs[:, b, j], in_=w_t[:].rearrange("p i u m -> p i m u"))
-                    else:
-                        nc.vector.tensor_copy(out=pairs[:, b, j], in_=w_t[:].rearrange("p i u m -> p i m u"))
-            width = 2 * PIXELS * PACK
-            for b in range(BANKS_PER_TILE):
-                nc.vector.quantize_mx(
-                    out=codes[:, 2 * b : 2 * b + 2, :].rearrange("p g m -> p (g m)").bitcast(FP8X4),
-                    scales=scales[:, 2 * b : 2 * b + 2, :].rearrange("p g m -> p (g m)"),
-                    in_=grouped[:, b * width : (b + 1) * width],
-                )
-            w_codes[n] = codes
-            w_scales[n] = scales
 
-        agg_grouped = {}
-        agg_bank = {}
-
-        def aggregate(n, feature_tiles):
-            for t in feature_tiles:
-                h, s = divmod(t, 2)
-                if t == 0:
-                    agg_grouped[n] = agg_work.tile([P, PIXELS, PACK], BF16, align_bytes=64, name="agg_grouped")
-                if s == 0:
-                    agg_bank[n] = psum_agg.tile([P, 2, PIXELS], F32, name="agg_t")
-                for g in range(NODE_PASSES):
-                    nc.tensor.matmul_mx(
-                        out=agg_bank[n][:, s, :],
-                        lhsT=hid_codes[:, g, t * P : (t + 1) * P].bitcast(FP8X4),
-                        lhsT_scale=hid_scales[:, g, t * P : (t + 1) * P],
-                        rhs=w_codes[n][:, g, :].bitcast(FP8X4),
-                        rhs_scale=w_scales[n][:, g, :],
-                        start=(g == 0),
-                        stop=(g == NODE_PASSES - 1),
-                    )
-                if s == 1:
-                    nc.scalar.copy(
-                        out=agg_grouped[n][:, :, 2 * h : 2 * h + 2], in_=agg_bank[n][:].rearrange("p s m -> p m s")
-                    )
-
-        def quantise_agg(n):
-            codes = agg_work.tile([P, PIXELS], U32, align_bytes=64, name="agg_codes")
-            scales = agg_work.tile([P, PIXELS], U8, align_bytes=64, name="agg_scales")
+        def quantise_weight(n, g):
             nc.vector.quantize_mx(
-                out=codes[:].bitcast(FP8X4), scales=scales[:], in_=agg_grouped[n][:].rearrange("p m t -> p (m t)")
+                out=w_codes[n][:, g : g + 2, :].rearrange("p g m -> p (g m)").bitcast(FP8X4),
+                scales=w_scales[n][:, g : g + 2, :].rearrange("p g m -> p (g m)"),
+                in_=w_grouped[n][:, g : g + 2, :, :].rearrange("p g m t -> p (g m t)"),
             )
-            agg_codes[n] = codes
-            agg_scales[n] = scales
 
-        def project(n):
-            y_t = psum_y.tile([P, OUT_TILES, PIXELS], F32, name="y_t")
+        def multiply(out_ap, t, n, m0, m1):
+            for g in range(NODE_PASSES):
+                nc.tensor.matmul_mx(
+                    out=out_ap,
+                    lhsT=hid_codes[:, g, t * P : (t + 1) * P].bitcast(FP8X4),
+                    lhsT_scale=hid_scales[:, g, t * P : (t + 1) * P],
+                    rhs=w_codes[n][:, g, m0:m1].bitcast(FP8X4),
+                    rhs_scale=w_scales[n][:, g, m0:m1],
+                    start=(g == 0),
+                    stop=(g == NODE_PASSES - 1),
+                )
+
+        def aggregate(n, h):
+            if n == LAST:
+                bank = psum_acc.tile([P, FEATURE_TILES, P], F32, tag="acc", name="agg_t")
+                for t in range(FEATURE_TILES):
+                    multiply(bank[:, t, :], t, n, h * P, (h + 1) * P)
+            else:
+                bank = psum_acc.tile([P, 2, PIXELS], F32, tag="acc", name="agg_t")
+                for s in range(2):
+                    multiply(bank[:, s, :], 2 * h + s, n, 0, PIXELS)
+            agg_banks[n, h] = bank
+
+        def copy_agg(n, h):
+            if h == 0:
+                agg_grouped[n] = agg_work.tile([P, PIXELS, PACK], BF16, align_bytes=64, name="agg_grouped")
+            if n == LAST:
+                nc.scalar.copy(
+                    out=agg_grouped[n][:, h * P : (h + 1) * P, :], in_=agg_banks[n, h][:].rearrange("p t m -> p m t")
+                )
+            else:
+                nc.scalar.copy(
+                    out=agg_grouped[n][:, :, 2 * h : 2 * h + 2], in_=agg_banks[n, h][:].rearrange("p s m -> p m s")
+                )
+
+        def quantise_agg(n, m0, m1):
+            if m0 == 0:
+                agg_codes[n] = agg_work.tile([P, PIXELS], U32, align_bytes=64, name="agg_codes")
+                agg_scales[n] = agg_work.tile([P, PIXELS], U8, align_bytes=64, name="agg_scales")
+            nc.vector.quantize_mx(
+                out=agg_codes[n][:, m0:m1].bitcast(FP8X4),
+                scales=agg_scales[n][:, m0:m1],
+                in_=agg_grouped[n][:, m0:m1, :].rearrange("p m t -> p (m t)"),
+            )
+
+        def project(n, m0, m1):
+            y_t = psum_acc.tile([P, OUT_TILES, m1 - m0], F32, tag="acc", name="y_t")
             for t_o in range(OUT_TILES):
                 nc.tensor.matmul_mx(
                     out=y_t[:, t_o, :],
                     lhsT=w2_codes[:, t_o * P : (t_o + 1) * P].bitcast(FP8X4),
                     lhsT_scale=w2_scales[:, t_o * P : (t_o + 1) * P],
-                    rhs=agg_codes[n][:].bitcast(FP8X4),
-                    rhs_scale=agg_scales[n][:],
+                    rhs=agg_codes[n][:, m0:m1].bitcast(FP8X4),
+                    rhs_scale=agg_scales[n][:, m0:m1],
                     start=True,
                     stop=True,
                 )
+            y_banks[n, m0] = y_t
+
+        def maximum(n, m0, m1):
             for t_o in range(OUT_TILES):
                 if n == 0:
                     nc.vector.tensor_scalar_add(
-                        out=y_max[:, t_o, :], in0=y_t[:, t_o, :], scalar1=bias[:, t_o : t_o + 1]
+                        out=y_max[:, t_o, m0:m1], in0=y_banks[n, m0][:, t_o, :], scalar1=bias[:, t_o : t_o + 1]
                     )
                 else:
                     nc.vector.scalar_tensor_tensor(
-                        out=y_max[:, t_o, :],
-                        in0=y_t[:, t_o, :],
+                        out=y_max[:, t_o, m0:m1],
+                        in0=y_banks[n, m0][:, t_o, :],
                         scalar=bias[:, t_o : t_o + 1],
-                        in1=y_max[:, t_o, :],
+                        in1=y_max[:, t_o, m0:m1],
                         op0=ADD,
                         op1=MAX,
                     )
 
+        for g in range(NODE_PASSES):
+            regroup_hid(g)
+            if g > 0:
+                quantise_hid(g - 1)
+        quantise_hid(NODE_PASSES - 1)
         transpose_weight(0)
+        for g in range(NODE_PASSES):
+            copy_weight(0, g)
+        quantise_weight(0, 0)
+        quantise_weight(0, 2)
+
         for n in range(SAMPLES):
-            aggregate(n, range(0, LEAD))
-            if n + 1 < SAMPLES:
+            if n > 0:
+                copy_agg(n - 1, 1)
+            if n < LAST:
                 transpose_weight(n + 1)
+                copy_weight(n + 1, 0)
+                copy_weight(n + 1, 1)
+            if n > 1:
+                maximum(n - 2, 0, PIXELS)
+            if n > 0:
+                quantise_agg(n - 1, 0, PIXELS)
+            if n < LAST:
+                copy_weight(n + 1, 2)
+                copy_weight(n + 1, 3)
+                quantise_weight(n + 1, 0)
+                quantise_weight(n + 1, 2)
             if n == 0:
                 prepare_w2()
-            aggregate(n, range(LEAD, FEATURE_TILES))
+            aggregate(n, 0)
+            copy_agg(n, 0)
+            aggregate(n, 1)
             if n > 0:
-                project(n - 1)
-            quantise_agg(n)
-        project(SAMPLES - 1)
+                project(n - 1, 0, PIXELS)
+        copy_agg(LAST, 1)
+        maximum(LAST - 1, 0, PIXELS)
 
-        result = const.tile([P, OUT_TILES, PIXELS], F32)
-        nc.vector.scalar_tensor_tensor(
-            out=result[:].rearrange("p t m -> p (t m)"),
-            in0=y_max[:].rearrange("p t m -> p (t m)"),
-            scalar=SLOPE,
-            in1=y_max[:].rearrange("p t m -> p (t m)"),
-            op0=MULT,
-            op1=MAX,
-        )
-        nc.sync.dma_start(out=out[0].rearrange("(t p) h w -> p t (h w)", p=P), in_=result[:])
-
-
-def quantise_hid(nc, hid_grouped, hid_codes, hid_scales, g):
-    nc.vector.quantize_mx(
-        out=hid_codes[:, g, :].bitcast(FP8X4),
-        scales=hid_scales[:, g, :],
-        in_=hid_grouped[:, g, :, :].rearrange("p f t -> p (f t)"),
-    )
+        spans = [(h * P, (h + 1) * P) for h in range(ROW_TILES)]
+        for m0, m1 in spans:
+            quantise_agg(LAST, m0, m1)
+        for m0, m1 in spans:
+            project(LAST, m0, m1)
+        for m0, m1 in spans:
+            maximum(LAST, m0, m1)
+        for m0, m1 in spans:
+            nc.vector.scalar_tensor_tensor(
+                out=result[:, :, m0:m1],
+                in0=y_max[:, :, m0:m1],
+                scalar=SLOPE,
+                in1=y_max[:, :, m0:m1],
+                op0=MULT,
+                op1=MAX,
+            )
+            nc.sync.dma_start(
+                out=out[0].rearrange("(t p) h w -> p t (h w)", p=P)[:, :, m0:m1], in_=result[:, :, m0:m1]
+            )

@@ -26,6 +26,7 @@ OUT_TILES = OUT // P
 HALVES = 2
 LAST = SAMPLES - 1
 SLOPE = 0.01
+WARM = (3, 2, 2, 2)
 COPIERS = "SVSV"
 
 FLOPS = 2 * NODES * NODES * HIDDEN + 2 * NODES * HIDDEN * OUT
@@ -228,6 +229,12 @@ def tile_similargcn_pb_kernel(tc, weight, hid, W2, b2, out):
                         op1=MAX,
                     )
 
+        warm = psum_acc.tile([P, HIDDEN], F32, tag="acc", name="warm")
+        for g in range(NODE_PASSES):
+            for i in range(WARM[g]):
+                nc.tensor.matmul(
+                    out=warm[:], lhsT=hid_raw[:, g, i, 0:P], rhs=hid_raw[:, g, i, :], start=True, stop=True
+                )
         for g in range(NODE_PASSES):
             regroup_hid(g)
             if g > 0:

@@ -60,14 +60,9 @@ def tile_similargcn_pb_kernel(tc, weight, hid, W2, b2, out):
         w_raw = []
         for n in range(SAMPLES):
             rows = w_in.tile([P, ROW_TILES, NODES], BF16, name="w_raw")
-            chunks = 2 if n < 2 else 1
-            width = NODES // chunks
-            for c in range(chunks):
-                cols = slice(c * width, (c + 1) * width)
-                nc.sync.dma_start(
-                    out=rows[:, :, cols],
-                    in_=weight[n * PIXELS : (n + 1) * PIXELS, cols].rearrange("(j p) k -> p j k", p=P),
-                )
+            nc.sync.dma_start(
+                out=rows[:], in_=weight[n * PIXELS : (n + 1) * PIXELS, :].rearrange("(p j) k -> p j k", p=P)
+            )
             w_raw.append(rows)
             if n == 1:
                 nc.sync.dma_start(out=w2_raw[:], in_=W2.rearrange("(t p) f -> p t f", p=P))
@@ -143,8 +138,8 @@ def tile_similargcn_pb_kernel(tc, weight, hid, W2, b2, out):
             grouped = w_grouped[n][:, g, :, :].rearrange("p m t -> p (m t)").bitcast(F32)
             copy = nc.scalar.copy if COPIERS[g] == "S" else nc.vector.tensor_copy
             copy(
-                out=grouped.rearrange("p (j m u) -> p j m u", j=ROW_TILES, u=HALVES),
-                in_=w_banks[n, g][:].rearrange("p j u m -> p j m u"),
+                out=grouped.rearrange("p (m j u) -> p m j u", j=ROW_TILES, u=HALVES),
+                in_=w_banks[n, g][:].rearrange("p j u m -> p m j u"),
             )
 
         def quantise_weight(n, g):

@@ -25,9 +25,11 @@ FEATURE_TILES = HIDDEN // P
 OUT_TILES = OUT // P
 HALVES = 2
 LAST = SAMPLES - 1
+BLOCK = 32
+BLOCKS = PIXELS * HALVES // BLOCK
 SLOPE = 0.01
 WARM = (3, 2, 2, 2)
-COPIERS = "SVSV"
+COPIERS = ("SVSV",) * 4 + ("SVSS",) * 3
 
 FLOPS = 2 * NODES * NODES * HIDDEN + 2 * NODES * HIDDEN * OUT
 
@@ -58,7 +60,20 @@ def tile_similargcn_pb_kernel(tc, weight, hid, W2, b2, out):
         bias_rows = const.tile([P, P], BF16)
         nc.vector.memset(bias_rows[:], 0.0)
         w_raw = []
-        for n in range(SAMPLES):
+        last_raw = [const.tile([P, BLOCKS, 2 * BLOCK], BF16, align_bytes=64, name="last_%d" % g) for g in range(NODE_PASSES)]
+
+        def load_last(g):
+            for q in range(P // BLOCK):
+                for u in range(HALVES):
+                    k0 = g * K_PASS + u * (K_PASS // HALVES) + q * 2 * BLOCK
+                    nc.sync.dma_start(
+                        out=last_raw[g][q * BLOCK + u : (q + 1) * BLOCK : HALVES, :, :],
+                        in_=weight[LAST * PIXELS : (LAST + 1) * PIXELS, k0 : k0 + 2 * BLOCK].rearrange(
+                            "(a r) k -> r a k", a=BLOCKS
+                        ),
+                    )
+
+        for n in range(LAST):
             rows = w_in.tile([P, ROW_TILES, NODES], BF16, name="w_raw")
             nc.sync.dma_start(
                 out=rows[:], in_=weight[n * PIXELS : (n + 1) * PIXELS, :].rearrange("(p j) k -> p j k", p=P)
@@ -67,6 +82,8 @@ def tile_similargcn_pb_kernel(tc, weight, hid, W2, b2, out):
             if n == 1:
                 nc.sync.dma_start(out=w2_raw[:], in_=W2.rearrange("(t p) f -> p t f", p=P))
                 nc.sync.dma_start(out=bias_rows[0:OUT_TILES, :], in_=b2.rearrange("(t o) -> t o", t=OUT_TILES))
+        for g in range(NODE_PASSES):
+            load_last(g)
 
         hid_grouped = const.tile([P, NODE_PASSES, HIDDEN, PACK], BF16, align_bytes=64)
         hid_codes = const.tile([P, NODE_PASSES, HIDDEN], U32, align_bytes=64)
@@ -134,9 +151,20 @@ def tile_similargcn_pb_kernel(tc, weight, hid, W2, b2, out):
                         nc.tensor.transpose(w_t[:, j, u, :], words[:, c0 : c0 + P], ident_f32[:])
                 w_banks[n, g] = w_t
 
+        def start_last():
+            w_grouped[LAST] = const.tile([P, NODE_PASSES, PIXELS, PACK], BF16, align_bytes=64, name="last_grouped")
+            w_codes[LAST] = const.tile([P, NODE_PASSES, PIXELS], U32, align_bytes=64, name="last_codes")
+            w_scales[LAST] = const.tile([P, NODE_PASSES, PIXELS], U8, align_bytes=64, name="last_scales")
+
+        def turn_last(g):
+            nc.vector.transpose(
+                w_grouped[LAST][:, g, :, :].rearrange("p m t -> p (m t)").bitcast(F32),
+                last_raw[g][:].rearrange("p a i -> p (a i)").bitcast(F32),
+            )
+
         def copy_weight(n, g):
             grouped = w_grouped[n][:, g, :, :].rearrange("p m t -> p (m t)").bitcast(F32)
-            copy = nc.scalar.copy if COPIERS[g] == "S" else nc.vector.tensor_copy
+            copy = nc.scalar.copy if COPIERS[n][g] == "S" else nc.vector.tensor_copy
             copy(
                 out=grouped.rearrange("p (m j u) -> p m j u", j=ROW_TILES, u=HALVES),
                 in_=w_banks[n, g][:].rearrange("p j u m -> p m j u"),
@@ -241,22 +269,33 @@ def tile_similargcn_pb_kernel(tc, weight, hid, W2, b2, out):
         quantise_weight(0, 0)
         quantise_weight(0, 2)
 
+        first_turn = LAST - NODE_PASSES
         for n in range(SAMPLES):
             if n > 0:
                 copy_agg(n - 1, 1)
-            if n < LAST:
+            if n + 1 < LAST:
                 transpose_weight(n + 1)
                 copy_weight(n + 1, 0)
                 copy_weight(n + 1, 1)
+            if n == LAST - 1:
+                quantise_agg(n - 1, 0, PIXELS)
+                quantise_weight(LAST, 2)
             if n > 1:
                 maximum(n - 2, 0, PIXELS)
-            if n > 0:
+            if n > 0 and n != LAST - 1:
                 quantise_agg(n - 1, 0, PIXELS)
-            if n < LAST:
+            if n + 1 < LAST:
                 copy_weight(n + 1, 2)
                 copy_weight(n + 1, 3)
                 quantise_weight(n + 1, 0)
                 quantise_weight(n + 1, 2)
+            if n == first_turn:
+                start_last()
+            if first_turn <= n < LAST - 1:
+                turn_last(n - first_turn)
+            if n == LAST - 2:
+                turn_last(NODE_PASSES - 1)
+                quantise_weight(LAST, 0)
             if n == 0:
                 prepare_w2()
             aggregate(n, 0)

@@ -25,11 +25,12 @@ FEATURE_TILES = HIDDEN // P
 OUT_TILES = OUT // P
 HALVES = 2
 LAST = SAMPLES - 1
+PAIR_COPIERS = "SVSV"
+PAIR = 2
 BLOCK = 32
 BLOCKS = PIXELS * HALVES // BLOCK
 SLOPE = 0.01
-WARM = (3, 2, 2, 2)
-COPIERS = ("SVSV",) * 4 + ("SVSS",) * 3
+COPIERS = ("SSSV",) * 2 + ("SVSS",) * 5
 
 FLOPS = 2 * NODES * NODES * HIDDEN + 2 * NODES * HIDDEN * OUT
 
@@ -51,15 +52,30 @@ def tile_similargcn_pb_kernel(tc, weight, hid, W2, b2, out):
         make_identity(nc, ident_bf16[:])
 
         hid_raw = const.tile([P, NODE_PASSES, PACK, HIDDEN], BF16)
-        for g in range(NODE_PASSES):
+
+        def load_hid(g):
             nc.sync.dma_start(
                 out=hid_raw[:, g, :, :].rearrange("p (u e) f -> p u e f", u=HALVES),
                 in_=hid[g * K_PASS : (g + 1) * K_PASS, :].rearrange("(u p e) f -> p u e f", u=HALVES, p=P),
             )
+
+        w_raw = []
+
+        def load_weight(n):
+            rows = w_in.tile([P, ROW_TILES, NODES], BF16, name="w_raw")
+            nc.sync.dma_start(
+                out=rows[:], in_=weight[n * PIXELS : (n + 1) * PIXELS, :].rearrange("(p j) k -> p j k", p=P)
+            )
+            w_raw.append(rows)
+
         w2_raw = const.tile([P, OUT_TILES, HIDDEN], BF16)
         bias_rows = const.tile([P, P], BF16)
         nc.vector.memset(bias_rows[:], 0.0)
-        w_raw = []
+
+        def load_w2():
+            nc.sync.dma_start(out=w2_raw[:], in_=W2.rearrange("(t p) f -> p t f", p=P))
+            nc.sync.dma_start(out=bias_rows[0:OUT_TILES, :], in_=b2.rearrange("(t o) -> t o", t=OUT_TILES))
+
         last_raw = [const.tile([P, BLOCKS, 2 * BLOCK], BF16, align_bytes=64, name="last_%d" % g) for g in range(NODE_PASSES)]
 
         def load_last(g):
@@ -73,18 +89,22 @@ def tile_similargcn_pb_kernel(tc, weight, hid, W2, b2, out):
                         ),
                     )
 
-        for n in range(LAST):
-            rows = w_in.tile([P, ROW_TILES, NODES], BF16, name="w_raw")
-            nc.sync.dma_start(
-                out=rows[:], in_=weight[n * PIXELS : (n + 1) * PIXELS, :].rearrange("(p j) k -> p j k", p=P)
-            )
-            w_raw.append(rows)
-            if n == 1:
-                nc.sync.dma_start(out=w2_raw[:], in_=W2.rearrange("(t p) f -> p t f", p=P))
-                nc.sync.dma_start(out=bias_rows[0:OUT_TILES, :], in_=b2.rearrange("(t o) -> t o", t=OUT_TILES))
-        for g in range(NODE_PASSES):
-            load_last(g)
-
+        load_hid(0)
+        load_weight(0)
+        load_weight(1)
+        load_hid(1)
+        load_w2()
+        load_hid(2)
+        load_hid(3)
+        load_weight(2)
+        load_weight(3)
+        load_weight(4)
+        load_last(0)
+        load_weight(5)
+        load_last(1)
+        load_weight(6)
+        load_last(2)
+        load_last(3)
         hid_grouped = const.tile([P, NODE_PASSES, HIDDEN, PACK], BF16, align_bytes=64)
         hid_codes = const.tile([P, NODE_PASSES, HIDDEN], U32, align_bytes=64)
         hid_scales = const.tile([P, NODE_PASSES, HIDDEN], U8, align_bytes=64)
@@ -122,26 +142,81 @@ def tile_similargcn_pb_kernel(tc, weight, hid, W2, b2, out):
         agg_scales = {}
         y_banks = {}
 
-        def prepare_w2():
+        w2_banks = []
+        w2_grouped = const.tile([P, OUT_TILES, P, PACK], BF16, align_bytes=64)
+
+        def prepare_w2_transposes():
             w2_t = psum_wt.tile([P, OUT_TILES, FEATURE_TILES, P], BF16, tag="w_t")
             for t_o in range(OUT_TILES):
                 for t in range(FEATURE_TILES):
                     nc.tensor.transpose(w2_t[:, t_o, t, :], w2_raw[:, t_o, t * P : (t + 1) * P], ident_bf16[:])
             bias_t = psum_wt.tile([P, P], BF16, tag="w_t")
             nc.tensor.transpose(bias_t[:], bias_rows[:], ident_bf16[:])
-            w2_grouped = const.tile([P, OUT_TILES, P, PACK], BF16, align_bytes=64)
-            nc.vector.tensor_copy(out=w2_grouped[:], in_=w2_t[:].rearrange("p a t o -> p a o t"))
+            w2_banks.extend([w2_t, bias_t])
+
+        def prepare_w2_words():
+            w2_t, bias_t = w2_banks
+            nc.scalar.copy(out=w2_grouped[:], in_=w2_t[:].rearrange("p a t o -> p a o t"))
             nc.vector.tensor_copy(out=bias[:], in_=bias_t[:, 0:OUT_TILES])
+
+        def quantise_w2():
             nc.vector.quantize_mx(
                 out=w2_codes[:].bitcast(FP8X4),
                 scales=w2_scales[:],
                 in_=w2_grouped[:].rearrange("p a o t -> p (a o t)"),
             )
 
+        warm = psum_acc.tile([P, HIDDEN], F32, tag="acc", name="warm")
+
+        def keep_busy(rows, count):
+            for i in range(count):
+                nc.tensor.matmul(out=warm[:], lhsT=rows[:, 0:P], rhs=rows, start=True, stop=True)
+
+        pair_grouped = const.tile([P, NODE_PASSES, PAIR * PIXELS, PACK], BF16, align_bytes=64)
+        pair_codes = const.tile([P, NODE_PASSES, PAIR * PIXELS], U32, align_bytes=64)
+        pair_scales = const.tile([P, NODE_PASSES, PAIR * PIXELS], U8, align_bytes=64)
+        pair_banks = []
+        pair_rows = const.tile([P, FEATURE_TILES, PAIR * PIXELS], BF16)
+
+        def quantise_pair(g):
+            nc.vector.quantize_mx(
+                out=pair_codes[:, g, :].bitcast(FP8X4),
+                scales=pair_scales[:, g, :],
+                in_=pair_grouped[:, g, :, :].rearrange("p m t -> p (m t)"),
+            )
+
+        def multiply_pair(g):
+            for t in range(FEATURE_TILES):
+                if g == 0:
+                    pair_banks.append(psum_acc.tile([P, PAIR * PIXELS], F32, tag="acc", name="pair_t"))
+                nc.tensor.matmul_mx(
+                    out=pair_banks[t][:],
+                    lhsT=hid_codes[:, g, t * P : (t + 1) * P].bitcast(FP8X4),
+                    lhsT_scale=hid_scales[:, g, t * P : (t + 1) * P],
+                    rhs=pair_codes[:, g, :].bitcast(FP8X4),
+                    rhs_scale=pair_scales[:, g, :],
+                    start=(g == 0),
+                    stop=(g == NODE_PASSES - 1),
+                )
+
+        def copy_pair(t):
+            copy = nc.scalar.copy if PAIR_COPIERS[t] == "S" else nc.vector.tensor_copy
+            copy(out=pair_rows[:, t, :], in_=pair_banks[t][:])
+
+        def group_pair(n):
+            agg_grouped[n] = agg_work.tile([P, PIXELS, PACK], BF16, align_bytes=64, name="agg_grouped")
+            nc.vector.tensor_copy(
+                out=agg_grouped[n][:].rearrange("p (c i) t -> p c t i", i=4),
+                in_=pair_rows[:, :, n * PIXELS : (n + 1) * PIXELS].rearrange("p t (c i) -> p c t i", i=4),
+            )
+
         def transpose_weight(n):
-            w_grouped[n] = w_work.tile([P, NODE_PASSES, PIXELS, PACK], BF16, align_bytes=64, name="w_grouped")
-            w_codes[n] = w_work.tile([P, NODE_PASSES, PIXELS], U32, align_bytes=64, name="w_codes")
-            w_scales[n] = w_work.tile([P, NODE_PASSES, PIXELS], U8, align_bytes=64, name="w_scales")
+            if n < PAIR:
+                w_grouped[n] = pair_grouped[:, :, n * PIXELS : (n + 1) * PIXELS, :]
+            else:
+                w_grouped[n] = w_work.tile([P, NODE_PASSES, PIXELS, PACK], BF16, align_bytes=64, name="w_grouped")
+                w_codes[n] = w_work.tile([P, NODE_PASSES, PIXELS], U32, align_bytes=64, name="w_codes")
+                w_scales[n] = w_work.tile([P, NODE_PASSES, PIXELS], U8, align_bytes=64, name="w_scales")
             for g in range(NODE_PASSES):
                 w_t = psum_wt.tile([P, ROW_TILES, HALVES, P], F32, name="w_t")
                 for j in range(ROW_TILES):
@@ -252,27 +327,59 @@ def tile_similargcn_pb_kernel(tc, weight, hid, W2, b2, out):
                         op1=MAX,
                     )
 
-        warm = psum_acc.tile([P, HIDDEN], F32, tag="acc", name="warm")
-        for g in range(NODE_PASSES):
-            for i in range(WARM[g]):
-                nc.tensor.matmul(
-                    out=warm[:], lhsT=hid_raw[:, g, i, 0:P], rhs=hid_raw[:, g, i, :], start=True, stop=True
-                )
-        for g in range(NODE_PASSES):
-            regroup_hid(g)
-            if g > 0:
-                quantise_hid(g - 1)
-        quantise_hid(NODE_PASSES - 1)
+        regroup_hid(0)
+        keep_busy(hid_raw[:, 0, 0, :], 4)
+        quantise_hid(0)
         transpose_weight(0)
+        keep_busy(w_raw[0][:, 0, 0:HIDDEN], 2)
         for g in range(NODE_PASSES):
             copy_weight(0, g)
-        quantise_weight(0, 0)
-        quantise_weight(0, 2)
+        transpose_weight(1)
+        keep_busy(w_raw[1][:, 0, 0:HIDDEN], 2)
+        copy_weight(1, 0)
+        quantise_pair(0)
+        copy_weight(1, 1)
+        copy_weight(1, 2)
+        regroup_hid(1)
+        quantise_pair(1)
+        quantise_hid(1)
+        copy_weight(1, 3)
+        multiply_pair(0)
+        prepare_w2_transposes()
+        regroup_hid(2)
+        quantise_pair(2)
+        quantise_hid(2)
+        multiply_pair(1)
+        regroup_hid(3)
+        prepare_w2_words()
+        transpose_weight(2)
+        quantise_pair(3)
+        quantise_hid(3)
+        multiply_pair(2)
+        multiply_pair(3)
+        for g in range(NODE_PASSES):
+            copy_weight(2, g)
+        quantise_weight(2, 0)
+        quantise_weight(2, 2)
+        for t in range(FEATURE_TILES):
+            copy_pair(t)
+        transpose_weight(3)
+        for g in range(NODE_PASSES):
+            copy_weight(3, g)
+        group_pair(0)
+        group_pair(1)
+        quantise_weight(3, 0)
+        quantise_weight(3, 2)
+        aggregate(2, 0)
+        copy_agg(2, 0)
+        quantise_agg(0, 0, PIXELS)
+        quantise_agg(1, 0, PIXELS)
+        aggregate(2, 1)
+        quantise_w2()
 
         first_turn = LAST - NODE_PASSES
-        for n in range(SAMPLES):
-            if n > 0:
-                copy_agg(n - 1, 1)
+        for n in range(3, SAMPLES):
+            copy_agg(n - 1, 1)
             if n + 1 < LAST:
                 transpose_weight(n + 1)
                 copy_weight(n + 1, 0)
@@ -280,9 +387,9 @@ def tile_similargcn_pb_kernel(tc, weight, hid, W2, b2, out):
             if n == LAST - 1:
                 quantise_agg(n - 1, 0, PIXELS)
                 quantise_weight(LAST, 2)
-            if n > 1:
+            if n > 3:
                 maximum(n - 2, 0, PIXELS)
-            if n > 0 and n != LAST - 1:
+            if n != LAST - 1:
                 quantise_agg(n - 1, 0, PIXELS)
             if n + 1 < LAST:
                 copy_weight(n + 1, 2)
@@ -296,24 +403,25 @@ def tile_similargcn_pb_kernel(tc, weight, hid, W2, b2, out):
             if n == LAST - 2:
                 turn_last(NODE_PASSES - 1)
                 quantise_weight(LAST, 0)
-            if n == 0:
-                prepare_w2()
             aggregate(n, 0)
             copy_agg(n, 0)
-            aggregate(n, 1)
-            if n > 0:
+            if n == LAST:
                 project(n - 1, 0, PIXELS)
-        copy_agg(LAST, 1)
-        maximum(LAST - 1, 0, PIXELS)
+            aggregate(n, 1)
+            if n == 3:
+                project(0, 0, PIXELS)
+                project(1, 0, PIXELS)
+                maximum(0, 0, PIXELS)
+                maximum(1, 0, PIXELS)
+            if n < LAST:
+                project(n - 1, 0, PIXELS)
+        def last_copy(copy, m0, m1):
+            copy(
+                out=agg_grouped[LAST][:, m0:m1, :],
+                in_=agg_banks[LAST, 1][:, :, m0 - P : m1 - P].rearrange("p t m -> p m t"),
+            )
 
-        spans = [(h * P, (h + 1) * P) for h in range(ROW_TILES)]
-        for m0, m1 in spans:
-            quantise_agg(LAST, m0, m1)
-        for m0, m1 in spans:
-            project(LAST, m0, m1)
-        for m0, m1 in spans:
-            maximum(LAST, m0, m1)
-        for m0, m1 in spans:
+        def finish(m0, m1):
             nc.vector.scalar_tensor_tensor(
                 out=result[:, :, m0:m1],
                 in0=y_max[:, :, m0:m1],
@@ -325,3 +433,15 @@ def tile_similargcn_pb_kernel(tc, weight, hid, W2, b2, out):
             nc.sync.dma_start(
                 out=out[0].rearrange("(t p) h w -> p t (h w)", p=P)[:, :, m0:m1], in_=result[:, :, m0:m1]
             )
+
+        quantise_agg(LAST, 0, P)
+        maximum(LAST - 1, 0, PIXELS)
+        project(LAST, 0, P)
+        last_copy(nc.scalar.copy, P, P + P // 2)
+        last_copy(nc.vector.tensor_copy, P + P // 2, PIXELS)
+        maximum(LAST, 0, P)
+        quantise_agg(LAST, P, PIXELS)
+        project(LAST, P, PIXELS)
+        finish(0, P)
+        maximum(LAST, P, PIXELS)
+        finish(P, PIXELS)

@@ -76,7 +76,7 @@ def tile_similargcn_pb_kernel(tc, weight, hid, W2, b2, out):
             nc.sync.dma_start(out=w2_raw[:], in_=W2.rearrange("(t p) f -> p t f", p=P))
             nc.sync.dma_start(out=bias_rows[0:OUT_TILES, :], in_=b2.rearrange("(t o) -> t o", t=OUT_TILES))
 
-        last_raw = [const.tile([P, BLOCKS, 2 * BLOCK], BF16, align_bytes=64, name="last_%d" % g) for g in range(NODE_PASSES)]
+        last_raw = [const.tile([P, BLOCKS, 2 * BLOCK], BF16, align_bytes=256, name="last_%d" % g) for g in range(NODE_PASSES)]
 
         def load_last(g):
             for q in range(P // BLOCK):
@@ -105,9 +105,9 @@ def tile_similargcn_pb_kernel(tc, weight, hid, W2, b2, out):
         load_weight(6)
         load_last(2)
         load_last(3)
-        hid_grouped = const.tile([P, NODE_PASSES, HIDDEN, PACK], BF16, align_bytes=64)
-        hid_codes = const.tile([P, NODE_PASSES, HIDDEN], U32, align_bytes=64)
-        hid_scales = const.tile([P, NODE_PASSES, HIDDEN], U8, align_bytes=64)
+        hid_grouped = const.tile([P, NODE_PASSES, HIDDEN, PACK], BF16, align_bytes=256)
+        hid_codes = const.tile([P, NODE_PASSES, HIDDEN], U32, align_bytes=256)
+        hid_scales = const.tile([P, NODE_PASSES, HIDDEN], U8, align_bytes=256)
         half = HIDDEN // 2
 
         def regroup_hid(g):
@@ -129,8 +129,8 @@ def tile_similargcn_pb_kernel(tc, weight, hid, W2, b2, out):
 
         y_max = const.tile([P, OUT_TILES, PIXELS], F32)
         bias = const.tile([P, OUT_TILES], F32)
-        w2_codes = const.tile([P, OUT], U32, align_bytes=64)
-        w2_scales = const.tile([P, OUT], U8, align_bytes=64)
+        w2_codes = const.tile([P, OUT], U32, align_bytes=256)
+        w2_scales = const.tile([P, OUT], U8, align_bytes=256)
         result = const.tile([P, OUT_TILES, PIXELS], F32)
         w_banks = {}
         w_grouped = {}
@@ -143,7 +143,7 @@ def tile_similargcn_pb_kernel(tc, weight, hid, W2, b2, out):
         y_banks = {}
 
         w2_banks = []
-        w2_grouped = const.tile([P, OUT_TILES, P, PACK], BF16, align_bytes=64)
+        w2_grouped = const.tile([P, OUT_TILES, P, PACK], BF16, align_bytes=256)
 
         def prepare_w2_transposes():
             w2_t = psum_wt.tile([P, OUT_TILES, FEATURE_TILES, P], BF16, tag="w_t")
@@ -172,9 +172,9 @@ def tile_similargcn_pb_kernel(tc, weight, hid, W2, b2, out):
             for i in range(count):
                 nc.tensor.matmul(out=warm[:], lhsT=rows[:, 0:P], rhs=rows, start=True, stop=True)
 
-        pair_grouped = const.tile([P, NODE_PASSES, PAIR * PIXELS, PACK], BF16, align_bytes=64)
-        pair_codes = const.tile([P, NODE_PASSES, PAIR * PIXELS], U32, align_bytes=64)
-        pair_scales = const.tile([P, NODE_PASSES, PAIR * PIXELS], U8, align_bytes=64)
+        pair_grouped = const.tile([P, NODE_PASSES, PAIR * PIXELS, PACK], BF16, align_bytes=256)
+        pair_codes = const.tile([P, NODE_PASSES, PAIR * PIXELS], U32, align_bytes=256)
+        pair_scales = const.tile([P, NODE_PASSES, PAIR * PIXELS], U8, align_bytes=256)
         pair_banks = []
         pair_rows = const.tile([P, FEATURE_TILES, PAIR * PIXELS], BF16)
 
@@ -204,7 +204,7 @@ def tile_similargcn_pb_kernel(tc, weight, hid, W2, b2, out):
             copy(out=pair_rows[:, t, :], in_=pair_banks[t][:])
 
         def group_pair(n):
-            agg_grouped[n] = agg_work.tile([P, PIXELS, PACK], BF16, align_bytes=64, name="agg_grouped")
+            agg_grouped[n] = agg_work.tile([P, PIXELS, PACK], BF16, align_bytes=256, name="agg_grouped")
             nc.vector.tensor_copy(
                 out=agg_grouped[n][:].rearrange("p (c i) t -> p c t i", i=4),
                 in_=pair_rows[:, :, n * PIXELS : (n + 1) * PIXELS].rearrange("p t (c i) -> p c t i", i=4),
@@ -214,9 +214,9 @@ def tile_similargcn_pb_kernel(tc, weight, hid, W2, b2, out):
             if n < PAIR:
                 w_grouped[n] = pair_grouped[:, :, n * PIXELS : (n + 1) * PIXELS, :]
             else:
-                w_grouped[n] = w_work.tile([P, NODE_PASSES, PIXELS, PACK], BF16, align_bytes=64, name="w_grouped")
-                w_codes[n] = w_work.tile([P, NODE_PASSES, PIXELS], U32, align_bytes=64, name="w_codes")
-                w_scales[n] = w_work.tile([P, NODE_PASSES, PIXELS], U8, align_bytes=64, name="w_scales")
+                w_grouped[n] = w_work.tile([P, NODE_PASSES, PIXELS, PACK], BF16, align_bytes=256, name="w_grouped")
+                w_codes[n] = w_work.tile([P, NODE_PASSES, PIXELS], U32, align_bytes=256, name="w_codes")
+                w_scales[n] = w_work.tile([P, NODE_PASSES, PIXELS], U8, align_bytes=256, name="w_scales")
             for g in range(NODE_PASSES):
                 w_t = psum_wt.tile([P, ROW_TILES, HALVES, P], F32, name="w_t")
                 for j in range(ROW_TILES):
@@ -227,9 +227,9 @@ def tile_similargcn_pb_kernel(tc, weight, hid, W2, b2, out):
                 w_banks[n, g] = w_t
 
         def start_last():
-            w_grouped[LAST] = const.tile([P, NODE_PASSES, PIXELS, PACK], BF16, align_bytes=64, name="last_grouped")
-            w_codes[LAST] = const.tile([P, NODE_PASSES, PIXELS], U32, align_bytes=64, name="last_codes")
-            w_scales[LAST] = const.tile([P, NODE_PASSES, PIXELS], U8, align_bytes=64, name="last_scales")
+            w_grouped[LAST] = const.tile([P, NODE_PASSES, PIXELS, PACK], BF16, align_bytes=256, name="last_grouped")
+            w_codes[LAST] = const.tile([P, NODE_PASSES, PIXELS], U32, align_bytes=256, name="last_codes")
+            w_scales[LAST] = const.tile([P, NODE_PASSES, PIXELS], U8, align_bytes=256, name="last_scales")
 
         def turn_last(g):
             nc.vector.transpose(
@@ -277,7 +277,7 @@ def tile_similargcn_pb_kernel(tc, weight, hid, W2, b2, out):
 
         def copy_agg(n, h):
             if h == 0:
-                agg_grouped[n] = agg_work.tile([P, PIXELS, PACK], BF16, align_bytes=64, name="agg_grouped")
+                agg_grouped[n] = agg_work.tile([P, PIXELS, PACK], BF16, align_bytes=256, name="agg_grouped")
             if n == LAST:
                 nc.scalar.copy(
                     out=agg_grouped[n][:, h * P : (h + 1) * P, :], in_=agg_banks[n, h][:].rearrange("p t m -> p m t")
@@ -289,8 +289,8 @@ def tile_similargcn_pb_kernel(tc, weight, hid, W2, b2, out):
 
         def quantise_agg(n, m0, m1):
             if m0 == 0:
-                agg_codes[n] = agg_work.tile([P, PIXELS], U32, align_bytes=64, name="agg_codes")
-                agg_scales[n] = agg_work.tile([P, PIXELS], U8, align_bytes=64, name="agg_scales")
+                agg_codes[n] = agg_work.tile([P, PIXELS], U32, align_bytes=256, name="agg_codes")
+                agg_scales[n] = agg_work.tile([P, PIXELS], U8, align_bytes=256, name="agg_scales")
             nc.vector.quantize_mx(
                 out=agg_codes[n][:, m0:m1].bitcast(FP8X4),
                 scales=agg_scales[n][:, m0:m1],
@@ -422,14 +422,15 @@ def tile_similargcn_pb_kernel(tc, weight, hid, W2, b2, out):
             )
 
         def finish(m0, m1):
-            nc.vector.scalar_tensor_tensor(
-                out=result[:, :, m0:m1],
-                in0=y_max[:, :, m0:m1],
-                scalar=SLOPE,
-                in1=y_max[:, :, m0:m1],
-                op0=MULT,
-                op1=MAX,
-            )
+            for t_o in range(OUT_TILES):
+                nc.vector.scalar_tensor_tensor(
+                    out=result[:, t_o, m0:m1],
+                    in0=y_max[:, t_o, m0:m1],
+                    scalar=SLOPE,
+                    in1=y_max[:, t_o, m0:m1],
+                    op0=MULT,
+                    op1=MAX,
+                )
             nc.sync.dma_start(
                 out=out[0].rearrange("(t p) h w -> p t (h w)", p=P)[:, :, m0:m1], in_=result[:, :, m0:m1]
             )

@@ -128,6 +128,7 @@ def tile_similargcn_pb_kernel(tc, weight, hid, W2, b2, out):
             )
 
         y_max = const.tile([P, OUT_TILES, PIXELS], F32)
+        y_all = const.tile([P, OUT_TILES, PIXELS], F32)
         bias = const.tile([P, OUT_TILES], F32)
         w2_codes = const.tile([P, OUT], U32, align_bytes=256)
         w2_scales = const.tile([P, OUT], U8, align_bytes=256)
@@ -241,8 +242,8 @@ def tile_similargcn_pb_kernel(tc, weight, hid, W2, b2, out):
             grouped = w_grouped[n][:, g, :, :].rearrange("p m t -> p (m t)").bitcast(F32)
             copy = nc.scalar.copy if COPIERS[n][g] == "S" else nc.vector.tensor_copy
             copy(
-                out=grouped.rearrange("p (m j u) -> p m j u", j=ROW_TILES, u=HALVES),
-                in_=w_banks[n, g][:].rearrange("p j u m -> p m j u"),
+                out=grouped.rearrange("p (j m u) -> p j m u", j=ROW_TILES, u=HALVES),
+                in_=w_banks[n, g][:].rearrange("p j u m -> p j m u"),
             )
 
         def quantise_weight(n, g):
@@ -421,13 +422,24 @@ def tile_similargcn_pb_kernel(tc, weight, hid, W2, b2, out):
                 in_=agg_banks[LAST, 1][:, :, m0 - P : m1 - P].rearrange("p t m -> p m t"),
             )
 
+        def last_maximum(m0, m1):
+            for t_o in range(OUT_TILES):
+                nc.vector.scalar_tensor_tensor(
+                    out=y_all[:, t_o, m0:m1].rearrange("p (m j) -> p m j", j=ROW_TILES),
+                    in0=y_banks[LAST, m0][:, t_o, :].rearrange("p (m j) -> p m j", j=ROW_TILES),
+                    scalar=bias[:, t_o : t_o + 1],
+                    in1=y_max[:, t_o, :].rearrange("p (j m) -> p m j", j=ROW_TILES)[:, m0 // ROW_TILES : m1 // ROW_TILES, :],
+                    op0=ADD,
+                    op1=MAX,
+                )
+
         def finish(m0, m1):
             for t_o in range(OUT_TILES):
                 nc.vector.scalar_tensor_tensor(
                     out=result[:, t_o, m0:m1],
-                    in0=y_max[:, t_o, m0:m1],
+                    in0=y_all[:, t_o, m0:m1],
                     scalar=SLOPE,
-                    in1=y_max[:, t_o, m0:m1],
+                    in1=y_all[:, t_o, m0:m1],
                     op0=MULT,
                     op1=MAX,
                 )
@@ -440,9 +452,9 @@ def tile_similargcn_pb_kernel(tc, weight, hid, W2, b2, out):
         project(LAST, 0, P)
         last_copy(nc.scalar.copy, P, P + P // 2)
         last_copy(nc.vector.tensor_copy, P + P // 2, PIXELS)
-        maximum(LAST, 0, P)
+        last_maximum(0, P)
         quantise_agg(LAST, P, PIXELS)
         project(LAST, P, PIXELS)
         finish(0, P)
-        maximum(LAST, P, PIXELS)
+        last_maximum(P, PIXELS)
         finish(P, PIXELS)

import concourse.mybir as mybir
from concourse.masks import make_identity

F32 = mybir.dt.float32
BF16 = mybir.dt.bfloat16
U32 = mybir.dt.uint32
U8 = mybir.dt.uint8
FP8X4 = mybir.dt.float8_e4m3fn_x4
ADD = mybir.AluOpType.add
MULT = mybir.AluOpType.mult
MAX = mybir.AluOpType.max

P = 128
PACK = 4
K_PASS = P * PACK

NODES = 2048
HIDDEN = 512
OUT = 256
SAMPLES = 8
PIXELS = NODES // SAMPLES
NODE_PASSES = NODES // K_PASS
ROW_TILES = PIXELS // P
FEATURE_TILES = HIDDEN // P
OUT_TILES = OUT // P
HALVES = 2
LAST = SAMPLES - 1
PAIR_COPIERS = "SVSV"
PAIR = 2
BLOCK = 32
BLOCKS = PIXELS * HALVES // BLOCK
SLOPE = 0.01
COPIERS = ("SSSV",) * 2 + ("SVSS",) * 5

FLOPS = 2 * NODES * NODES * HIDDEN + 2 * NODES * HIDDEN * OUT


def tile_similargcn_pb_kernel(tc, weight, hid, W2, b2, out):
    nc = tc.nc
    with (
        tc.manual_schedule(),
        tc.tile_pool(name="const", bufs=1) as const,
        tc.tile_pool(name="w_in", bufs=SAMPLES) as w_in,
        tc.tile_pool(name="w_work", bufs=3) as w_work,
        tc.tile_pool(name="agg_work", bufs=2) as agg_work,
        tc.psum_pool(name="psum_wt", bufs=4) as psum_wt,
        tc.psum_pool(name="psum_acc", bufs=4) as psum_acc,
    ):
        ident_f32 = const.tile([P, P], F32)
        make_identity(nc, ident_f32[:])
        ident_bf16 = const.tile([P, P], BF16)
        make_identity(nc, ident_bf16[:])

        hid_raw = const.tile([P, NODE_PASSES, PACK, HIDDEN], BF16)

        def load_hid(g):
            nc.sync.dma_start(
                out=hid_raw[:, g, :, :].rearrange("p (u e) f -> p u e f", u=HALVES),
                in_=hid[g * K_PASS : (g + 1) * K_PASS, :].rearrange("(u p e) f -> p u e f", u=HALVES, p=P),
            )

        w_raw = []

        def load_weight(n):
            rows = w_in.tile([P, ROW_TILES, NODES], BF16, name="w_raw")
            nc.sync.dma_start(
                out=rows[:], in_=weight[n * PIXELS : (n + 1) * PIXELS, :].rearrange("(p j) k -> p j k", p=P)
            )
            w_raw.append(rows)

        w2_raw = const.tile([P, OUT_TILES, HIDDEN], BF16)
        bias_rows = const.tile([P, P], BF16)
        nc.vector.memset(bias_rows[:], 0.0)

        def load_w2():
            nc.sync.dma_start(out=w2_raw[:], in_=W2.rearrange("(t p) f -> p t f", p=P))
            nc.sync.dma_start(out=bias_rows[0:OUT_TILES, :], in_=b2.rearrange("(t o) -> t o", t=OUT_TILES))

        last_raw = [const.tile([P, BLOCKS, 2 * BLOCK], BF16, align_bytes=256, name="last_%d" % g) for g in range(NODE_PASSES)]

        def load_last(g):
            for q in range(P // BLOCK):
                for u in range(HALVES):
                    k0 = g * K_PASS + u * (K_PASS // HALVES) + q * 2 * BLOCK
                    nc.sync.dma_start(
                        out=last_raw[g][q * BLOCK + u : (q + 1) * BLOCK : HALVES, :, :],
                        in_=weight[LAST * PIXELS : (LAST + 1) * PIXELS, k0 : k0 + 2 * BLOCK].rearrange(
                            "(a r) k -> r a k", a=BLOCKS
                        ),
                    )

        load_hid(0)
        load_weight(0)
        load_weight(1)
        load_hid(1)
        load_w2()
        load_hid(2)
        load_hid(3)
        load_weight(2)
        load_weight(3)
        load_weight(4)
        load_last(0)
        load_weight(5)
        load_last(1)
        load_weight(6)
        load_last(2)
        load_last(3)
        hid_grouped = const.tile([P, NODE_PASSES, HIDDEN, PACK], BF16, align_bytes=256)
        hid_codes = const.tile([P, NODE_PASSES, HIDDEN], U32, align_bytes=256)
        hid_scales = const.tile([P, NODE_PASSES, HIDDEN], U8, align_bytes=256)
        half = HIDDEN // 2

        def regroup_hid(g):
            nc.vector.tensor_copy(
                out=hid_grouped[:, g, 0:half, :].rearrange("p (c i) t -> p c t i", i=4),
                in_=hid_raw[:, g, :, 0:half].rearrange("p t (c i) -> p c t i", i=4),
            )
            nc.scalar.copy(
                out=hid_grouped[:, g, half:HIDDEN, :].rearrange("p (c i) t -> p c t i", i=4),
                in_=hid_raw[:, g, :, half:HIDDEN].rearrange("p t (c i) -> p c t i", i=4),
            )

        def quantise_hid(g):
            nc.vector.quantize_mx(
                out=hid_codes[:, g, :].bitcast(FP8X4),
                scales=hid_scales[:, g, :],
                in_=hid_grouped[:, g, :, :].rearrange("p f t -> p (f t)"),
            )

        y_max = const.tile([P, OUT_TILES, PIXELS], F32)
        y_all = const.tile([P, OUT_TILES, PIXELS], F32)
        bias = const.tile([P, OUT_TILES], F32)
        w2_codes = const.tile([P, OUT], U32, align_bytes=256)
        w2_scales = const.tile([P, OUT], U8, align_bytes=256)
        result = const.tile([P, OUT_TILES, PIXELS], F32)
        w_banks = {}
        w_grouped = {}
        w_codes = {}
        w_scales = {}
        agg_banks = {}
        agg_grouped = {}
        agg_codes = {}
        agg_scales = {}
        y_banks = {}

        w2_banks = []
        w2_grouped = const.tile([P, OUT_TILES, P, PACK], BF16, align_bytes=256)

        def prepare_w2_transposes():
            w2_t = psum_wt.tile([P, OUT_TILES, FEATURE_TILES, P], BF16, tag="w_t")
            for t_o in range(OUT_TILES):
                for t in range(FEATURE_TILES):
                    nc.tensor.transpose(w2_t[:, t_o, t, :], w2_raw[:, t_o, t * P : (t + 1) * P], ident_bf16[:])
            bias_t = psum_wt.tile([P, P], BF16, tag="w_t")
            nc.tensor.transpose(bias_t[:], bias_rows[:], ident_bf16[:])
            w2_banks.extend([w2_t, bias_t])

        def prepare_w2_words():
            w2_t, bias_t = w2_banks
            nc.scalar.copy(out=w2_grouped[:], in_=w2_t[:].rearrange("p a t o -> p a o t"))
            nc.vector.tensor_copy(out=bias[:], in_=bias_t[:, 0:OUT_TILES])

        def quantise_w2():
            nc.vector.quantize_mx(
                out=w2_codes[:].bitcast(FP8X4),
                scales=w2_scales[:],
                in_=w2_grouped[:].rearrange("p a o t -> p (a o t)"),
            )

        warm = psum_acc.tile([P, HIDDEN], F32, tag="acc", name="warm")

        def keep_busy(rows, count):
            for i in range(count):
                nc.tensor.matmul(out=warm[:], lhsT=rows[:, 0:P], rhs=rows, start=True, stop=True)

        pair_grouped = const.tile([P, NODE_PASSES, PAIR * PIXELS, PACK], BF16, align_bytes=256)
        pair_codes = const.tile([P, NODE_PASSES, PAIR * PIXELS], U32, align_bytes=256)
        pair_scales = const.tile([P, NODE_PASSES, PAIR * PIXELS], U8, align_bytes=256)
        pair_banks = []
        pair_rows = const.tile([P, FEATURE_TILES, PAIR * PIXELS], BF16)

        def quantise_pair(g):
            nc.vector.quantize_mx(
                out=pair_codes[:, g, :].bitcast(FP8X4),
                scales=pair_scales[:, g, :],
                in_=pair_grouped[:, g, :, :].rearrange("p m t -> p (m t)"),
            )

        def multiply_pair(g):
            for t in range(FEATURE_TILES):
                if g == 0:
                    pair_banks.append(psum_acc.tile([P, PAIR * PIXELS], F32, tag="acc", name="pair_t"))
                nc.tensor.matmul_mx(
                    out=pair_banks[t][:],
                    lhsT=hid_codes[:, g, t * P : (t + 1) * P].bitcast(FP8X4),
                    lhsT_scale=hid_scales[:, g, t * P : (t + 1) * P],
                    rhs=pair_codes[:, g, :].bitcast(FP8X4),
                    rhs_scale=pair_scales[:, g, :],
                    start=(g == 0),
                    stop=(g == NODE_PASSES - 1),
                )

        def copy_pair(t):
            copy = nc.scalar.copy if PAIR_COPIERS[t] == "S" else nc.vector.tensor_copy
            copy(out=pair_rows[:, t, :], in_=pair_banks[t][:])

        def group_pair(n):
            agg_grouped[n] = agg_work.tile([P, PIXELS, PACK], BF16, align_bytes=256, name="agg_grouped")
            nc.vector.tensor_copy(
                out=agg_grouped[n][:].rearrange("p (c i) t -> p c t i", i=4),
                in_=pair_rows[:, :, n * PIXELS : (n + 1) * PIXELS].rearrange("p t (c i) -> p c t i", i=4),
            )

        def transpose_weight(n):
            if n < PAIR:
                w_grouped[n] = pair_grouped[:, :, n * PIXELS : (n + 1) * PIXELS, :]
            else:
                w_grouped[n] = w_work.tile([P, NODE_PASSES, PIXELS, PACK], BF16, align_bytes=256, name="w_grouped")
                w_codes[n] = w_work.tile([P, NODE_PASSES, PIXELS], U32, align_bytes=256, name="w_codes")
                w_scales[n] = w_work.tile([P, NODE_PASSES, PIXELS], U8, align_bytes=256, name="w_scales")
            for g in range(NODE_PASSES):
                w_t = psum_wt.tile([P, ROW_TILES, HALVES, P], F32, name="w_t")
                for j in range(ROW_TILES):
                    words = w_raw[n][:, j, :].bitcast(F32)
                    for u in range(HALVES):
                        c0 = (g * HALVES + u) * P
                        nc.tensor.transpose(w_t[:, j, u, :], words[:, c0 : c0 + P], ident_f32[:])
                w_banks[n, g] = w_t

        def start_last():
            w_grouped[LAST] = const.tile([P, NODE_PASSES, PIXELS, PACK], BF16, align_bytes=256, name="last_grouped")
            w_codes[LAST] = const.tile([P, NODE_PASSES, PIXELS], U32, align_bytes=256, name="last_codes")
            w_scales[LAST] = const.tile([P, NODE_PASSES, PIXELS], U8, align_bytes=256, name="last_scales")

        def turn_last(g):
            nc.vector.transpose(
                w_grouped[LAST][:, g, :, :].rearrange("p m t -> p (m t)").bitcast(F32),
                last_raw[g][:].rearrange("p a i -> p (a i)").bitcast(F32),
            )

        def copy_weight(n, g):
            grouped = w_grouped[n][:, g, :, :].rearrange("p m t -> p (m t)").bitcast(F32)
            copy = nc.scalar.copy if COPIERS[n][g] == "S" else nc.vector.tensor_copy
            copy(
                out=grouped.rearrange("p (j m u) -> p j m u", j=ROW_TILES, u=HALVES),
                in_=w_banks[n, g][:].rearrange("p j u m -> p j m u"),
            )

        def quantise_weight(n, g):
            nc.vector.quantize_mx(
                out=w_codes[n][:, g : g + 2, :].rearrange("p g m -> p (g m)").bitcast(FP8X4),
                scales=w_scales[n][:, g : g + 2, :].rearrange("p g m -> p (g m)"),
                in_=w_grouped[n][:, g : g + 2, :, :].rearrange("p g m t -> p (g m t)"),
            )

        def multiply(out_ap, t, n, m0, m1):
            for g in range(NODE_PASSES):
                nc.tensor.matmul_mx(
                    out=out_ap,
                    lhsT=hid_codes[:, g, t * P : (t + 1) * P].bitcast(FP8X4),
                    lhsT_scale=hid_scales[:, g, t * P : (t + 1) * P],
                    rhs=w_codes[n][:, g, m0:m1].bitcast(FP8X4),
                    rhs_scale=w_scales[n][:, g, m0:m1],
                    start=(g == 0),
                    stop=(g == NODE_PASSES - 1),
                )

        def aggregate(n, h):
            if n == LAST:
                bank = psum_acc.tile([P, FEATURE_TILES, P], F32, tag="acc", name="agg_t")
                for t in range(FEATURE_TILES):
                    multiply(bank[:, t, :], t, n, h * P, (h + 1) * P)
            else:
                bank = psum_acc.tile([P, 2, PIXELS], F32, tag="acc", name="agg_t")
                for s in range(2):
                    multiply(bank[:, s, :], 2 * h + s, n, 0, PIXELS)
            agg_banks[n, h] = bank

        def copy_agg(n, h):
            if h == 0:
                agg_grouped[n] = agg_work.tile([P, PIXELS, PACK], BF16, align_bytes=256, name="agg_grouped")
            if n == LAST:
                nc.scalar.copy(
                    out=agg_grouped[n][:, h * P : (h + 1) * P, :], in_=agg_banks[n, h][:].rearrange("p t m -> p m t")
                )
            else:
                nc.scalar.copy(
                    out=agg_grouped[n][:, :, 2 * h : 2 * h + 2], in_=agg_banks[n, h][:].rearrange("p s m -> p m s")
                )

        def quantise_agg(n, m0, m1):
            if m0 == 0:
                agg_codes[n] = agg_work.tile([P, PIXELS], U32, align_bytes=256, name="agg_codes")
                agg_scales[n] = agg_work.tile([P, PIXELS], U8, align_bytes=256, name="agg_scales")
            nc.vector.quantize_mx(
                out=agg_codes[n][:, m0:m1].bitcast(FP8X4),
                scales=agg_scales[n][:, m0:m1],
                in_=agg_grouped[n][:, m0:m1, :].rearrange("p m t -> p (m t)"),
            )

        def project(n, m0, m1):
            y_t = psum_acc.tile([P, OUT_TILES, m1 - m0], F32, tag="acc", name="y_t")
            for t_o in range(OUT_TILES):
                nc.tensor.matmul_mx(
                    out=y_t[:, t_o, :],
                    lhsT=w2_codes[:, t_o * P : (t_o + 1) * P].bitcast(FP8X4),
                    lhsT_scale=w2_scales[:, t_o * P : (t_o + 1) * P],
                    rhs=agg_codes[n][:, m0:m1].bitcast(FP8X4),
                    rhs_scale=agg_scales[n][:, m0:m1],
                    start=True,
                    stop=True,
                )
            y_banks[n, m0] = y_t

        def maximum(n, m0, m1):
            for t_o in range(OUT_TILES):
                if n == 0:
                    nc.vector.tensor_scalar_add(
                        out=y_max[:, t_o, m0:m1], in0=y_banks[n, m0][:, t_o, :], scalar1=bias[:, t_o : t_o + 1]
                    )
                else:
                    nc.vector.scalar_tensor_tensor(
                        out=y_max[:, t_o, m0:m1],
                        in0=y_banks[n, m0][:, t_o, :],
                        scalar=bias[:, t_o : t_o + 1],
                        in1=y_max[:, t_o, m0:m1],
                        op0=ADD,
                        op1=MAX,
                    )

        regroup_hid(0)
        keep_busy(hid_raw[:, 0, 0, :], 4)
        quantise_hid(0)
        transpose_weight(0)
        keep_busy(w_raw[0][:, 0, 0:HIDDEN], 2)
        for g in range(NODE_PASSES):
            copy_weight(0, g)
        transpose_weight(1)
        keep_busy(w_raw[1][:, 0, 0:HIDDEN], 2)
        copy_weight(1, 0)
        quantise_pair(0)
        copy_weight(1, 1)
        copy_weight(1, 2)
        regroup_hid(1)
        quantise_pair(1)
        quantise_hid(1)
        copy_weight(1, 3)
        multiply_pair(0)
        prepare_w2_transposes()
        regroup_hid(2)
        quantise_pair(2)
        quantise_hid(2)
        multiply_pair(1)
        regroup_hid(3)
        prepare_w2_words()
        transpose_weight(2)
        quantise_pair(3)
        quantise_hid(3)
        multiply_pair(2)
        multiply_pair(3)
        for g in range(NODE_PASSES):
            copy_weight(2, g)
        quantise_weight(2, 0)
        quantise_weight(2, 2)
        for t in range(FEATURE_TILES):
            copy_pair(t)
        transpose_weight(3)
        for g in range(NODE_PASSES):
            copy_weight(3, g)
        group_pair(0)
        group_pair(1)
        quantise_weight(3, 0)
        quantise_weight(3, 2)
        aggregate(2, 0)
        copy_agg(2, 0)
        quantise_agg(0, 0, PIXELS)
        quantise_agg(1, 0, PIXELS)
        aggregate(2, 1)
        quantise_w2()

        first_turn = LAST - NODE_PASSES
        for n in range(3, SAMPLES):
            copy_agg(n - 1, 1)
            if n + 1 < LAST:
                transpose_weight(n + 1)
                copy_weight(n + 1, 0)
                copy_weight(n + 1, 1)
            if n == LAST - 1:
                quantise_agg(n - 1, 0, PIXELS)
                quantise_weight(LAST, 2)
            if n > 3:
                maximum(n - 2, 0, PIXELS)
            if n != LAST - 1:
                quantise_agg(n - 1, 0, PIXELS)
            if n + 1 < LAST:
                copy_weight(n + 1, 2)
                copy_weight(n + 1, 3)
                quantise_weight(n + 1, 0)
                quantise_weight(n + 1, 2)
            if n == first_turn:
                start_last()
            if first_turn <= n < LAST - 1:
                turn_last(n - first_turn)
            if n == LAST - 2:
                turn_last(NODE_PASSES - 1)
                quantise_weight(LAST, 0)
            aggregate(n, 0)
            copy_agg(n, 0)
            if n == LAST:
                project(n - 1, 0, PIXELS)
            aggregate(n, 1)
            if n == 3:
                project(0, 0, PIXELS)
                project(1, 0, PIXELS)
                maximum(0, 0, PIXELS)
                maximum(1, 0, PIXELS)
            if n < LAST:
                project(n - 1, 0, PIXELS)
        def last_copy(copy, m0, m1):
            copy(
                out=agg_grouped[LAST][:, m0:m1, :],
                in_=agg_banks[LAST, 1][:, :, m0 - P : m1 - P].rearrange("p t m -> p m t"),
            )

        def last_maximum(m0, m1):
            for t_o in range(OUT_TILES):
                nc.vector.scalar_tensor_tensor(
                    out=y_all[:, t_o, m0:m1].rearrange("p (m j) -> p m j", j=ROW_TILES),
                    in0=y_banks[LAST, m0][:, t_o, :].rearrange("p (m j) -> p m j", j=ROW_TILES),
                    scalar=bias[:, t_o : t_o + 1],
                    in1=y_max[:, t_o, :].rearrange("p (j m) -> p m j", j=ROW_TILES)[:, m0 // ROW_TILES : m1 // ROW_TILES, :],
                    op0=ADD,
                    op1=MAX,
                )

        def finish(m0, m1):
            for t_o in range(OUT_TILES):
                nc.vector.scalar_tensor_tensor(
                    out=result[:, t_o, m0:m1],
                    in0=y_all[:, t_o, m0:m1],
                    scalar=SLOPE,
                    in1=y_all[:, t_o, m0:m1],
                    op0=MULT,
                    op1=MAX,
                )
            nc.sync.dma_start(
                out=out[0].rearrange("(t p) h w -> p t (h w)", p=P)[:, :, m0:m1], in_=result[:, :, m0:m1]
            )

        quantise_agg(LAST, 0, P)
        maximum(LAST - 1, 0, PIXELS)
        project(LAST, 0, P)
        last_copy(nc.scalar.copy, P, P + P // 2)
        last_copy(nc.vector.tensor_copy, P + P // 2, PIXELS)
        last_maximum(0, P)
        quantise_agg(LAST, P, PIXELS)
        project(LAST, P, PIXELS)
        finish(0, P)
        last_maximum(P, PIXELS)
        finish(P, PIXELS)
